import numpy as np
import ml_dtypes


def mxq(x, axis, fmt="e4m3"):
    dtype, down = {"e4m3": (ml_dtypes.float8_e4m3fn, 7), "e5m2": (ml_dtypes.float8_e5m2, 14)}[fmt]
    v = np.moveaxis(np.asarray(x, np.float32).astype(ml_dtypes.bfloat16).astype(np.float64), axis, -1)
    blocks = v.reshape(v.shape[:-1] + (-1, 32))
    amax = np.abs(blocks).max(-1, keepdims=True)
    byte = np.maximum(np.where(amax > 0, np.frexp(amax)[1] - 1 + 127, 0) - down, 1)
    scale = np.exp2(byte - 127.0)
    codes = (blocks / scale).astype(np.float32).astype(dtype).astype(np.float64)
    return np.moveaxis((codes * scale).reshape(v.shape), -1, axis)


WIDE = False


def mx_kscale(k):
    if not WIDE:
        return np.ones(k)
    levels = np.array([10, -10, 5, -5, 0])
    a = np.random.permutation(np.resize(levels, k // 512 * 4)).reshape(k // 512, 4)
    idx = np.arange(k)
    return np.exp2(a[idx // 512, idx % 128 // 32])


BF16 = ml_dtypes.bfloat16


def bf(x):
    return np.asarray(x, np.float32).astype(BF16)


def f64(x):
    return np.asarray(x).astype(np.float64)


E2M1 = np.array([0.0, 0.5, 1.0, 1.5, 2.0, 3.0, 4.0, 6.0, -0.0, -0.5, -1.0, -1.5, -2.0, -3.0, -4.0, -6.0])


def pack_weight(w, fmt):
    k, n = w.shape
    w = f64(bf(w)).reshape(k // 32, 32, n)
    amax = np.abs(w).max(1)
    if fmt == "e4m3":
        byte = np.frexp(amax)[1] - 1 + 127 - 7
    else:
        mant, ex = np.frexp(amax / 6.0)
        byte = np.where(mant > 0.5, ex, ex - 1) + 127
    byte = np.clip(np.where(amax > 0, byte, 1), 1, 254)
    scaled = (w * np.exp2(127.0 - byte)[:, None, :]).reshape(k, n).astype(np.float32)
    by_word = np.ascontiguousarray(scaled.reshape(k // 512, 128, 4, n).transpose(0, 1, 3, 2))
    if fmt == "e4m3":
        words = by_word.astype(ml_dtypes.float8_e4m3fn).view(np.uint8)
    else:
        c = by_word.astype(ml_dtypes.float4_e2m1fn).view(np.uint8) & 0xF
        words = c[..., 0::2] | (c[..., 1::2] << 4)
    return np.ascontiguousarray(words), np.ascontiguousarray(byte.astype(np.uint8).reshape(k // 512, 16, n))


def unpack_weight(words, scales, fmt):
    g, p, n, _ = words.shape
    if fmt == "e4m3":
        vals = np.ascontiguousarray(words).view(ml_dtypes.float8_e4m3fn).astype(np.float64)
    else:
        nib = np.empty((g, p, n, 4), np.uint8)
        nib[..., 0::2] = words & 0xF
        nib[..., 1::2] = words >> 4
        vals = E2M1[nib]
    vals = vals * np.repeat(np.exp2(scales.astype(np.float64) - 127.0), 8, axis=1)[..., None]
    return vals.transpose(0, 1, 3, 2).reshape(g * 512, n)


B, N_VAR, D = 128, 8, 512
NUM_UNITS = N_VAR * D
ONE = 1


def sigmoid(v):
    return 1.0 / (1.0 + np.exp(-v))


def setup_inputs():
    s = mx_kscale(D)
    inputs = bf(np.random.standard_normal((B, N_VAR)))
    hidden = bf((np.random.standard_normal((B, D, N_VAR)) * s[None, :, None]).reshape(B, NUM_UNITS))
    gate_w_I2H = bf(np.random.standard_normal((N_VAR, 1, 2 * D, 1)) * 0.5)
    gate_stack = (np.random.standard_normal((N_VAR, 1, 2 * D, D)) / np.sqrt(D) / s).swapaxes(-1, -2)
    gate_words, gate_scales = pack_weight(gate_stack.reshape(-1, 2 * D), "e4m3")
    gate_bias = bf(np.random.standard_normal(2 * NUM_UNITS) * 0.4)
    update_w_I2H = bf(np.random.standard_normal((N_VAR, 1, D, 1)) * 0.5)
    update_stack = (np.random.standard_normal((N_VAR, 1, D, D)) * 1.5 / np.sqrt(D) / s).swapaxes(-1, -2)
    update_words, update_scales = pack_weight(update_stack.reshape(-1, D), "e4m3")
    update_bias = bf(np.random.standard_normal(NUM_UNITS) * 0.4)
    return {
        "inputs": inputs,
        "hidden": hidden,
        "gate_w_I2H": gate_w_I2H,
        "gate_w_H2H_words": gate_words,
        "gate_w_H2H_scales": gate_scales,
        "gate_bias": gate_bias,
        "update_w_I2H": update_w_I2H,
        "update_w_H2H_words": update_words,
        "update_w_H2H_scales": update_scales,
        "update_bias": update_bias,
    }


def reference(inputs, hidden, gate_w_I2H, gate_w_H2H_words, gate_w_H2H_scales, gate_bias, update_w_I2H, update_w_H2H_words, update_w_H2H_scales, update_bias):
    inputs, hidden = f64(inputs), f64(hidden)
    b, num_units = hidden.shape
    n_var = inputs.shape[1]
    d = num_units // n_var

    x_v = inputs.T
    h_v = hidden.reshape(b, d, n_var).transpose(2, 0, 1)

    gx = x_v[:, :, None] * f64(gate_w_I2H)[:, 0, :, 0][:, None, :]
    gh = mxq(h_v, 2, "e4m3") @ unpack_weight(gate_w_H2H_words, gate_w_H2H_scales, "e4m3").reshape(n_var, ONE, d, 2 * d)[:, 0]
    res_gate = (gx + gh).transpose(1, 0, 2).reshape(b, 2 * num_units) + f64(gate_bias)
    z, r = res_gate[:, :num_units], res_gate[:, num_units:]

    r_v = sigmoid(r).reshape(b, d, n_var).transpose(2, 0, 1)

    ux = x_v[:, :, None] * f64(update_w_I2H)[:, 0, :, 0][:, None, :]
    uh = mxq(h_v * r_v, 2, "e4m3") @ unpack_weight(update_w_H2H_words, update_w_H2H_scales, "e4m3").reshape(n_var, ONE, d, d)[:, 0]
    g = (ux + uh).transpose(1, 0, 2).reshape(b, num_units) + f64(update_bias)

    zs = sigmoid(z)
    return zs * hidden + (1.0 - zs) * np.tanh(g)

@@ -1,0 +1,258 @@
+from contextlib import ExitStack
+
+import concourse.mybir as mybir
+from concourse.masks import make_identity
+
+BF16 = mybir.dt.bfloat16
+F32 = mybir.dt.float32
+I32 = mybir.dt.int32
+U32 = mybir.dt.uint32
+U8 = mybir.dt.uint8
+FP8X4 = mybir.dt.float8_e4m3fn_x4
+ACT = mybir.ActivationFunctionType
+ALU = mybir.AluOpType
+
+P = 128
+N_VAR = 8
+D = 512
+PACK = 4
+UNITS = N_VAR * D
+BANK = 512
+N_BANKS = UNITS // BANK
+CHUNKS = BANK // P
+HALF = N_VAR // 2
+P_PER_BANK = BANK // (PACK * N_VAR)
+ONES_ROW = 16
+DEPTH = 2
+
+FLOPS = 2 * P * D * (3 * D) * N_VAR
+
+
+def tile_grucell_e_kernel(
+    tc,
+    inputs,
+    hidden,
+    gate_w_I2H,
+    gate_w_H2H_words,
+    gate_w_H2H_scales,
+    gate_bias,
+    update_w_I2H,
+    update_w_H2H_words,
+    update_w_H2H_scales,
+    update_bias,
+    out,
+):
+    nc = tc.nc
+    with ExitStack() as stack:
+        stack.enter_context(tc.manual_schedule())
+        keep = stack.enter_context(tc.tile_pool(name="keep", bufs=1))
+        work = stack.enter_context(tc.tile_pool(name="work", bufs=3))
+        psum_k = stack.enter_context(tc.psum_pool(name="psum_k", bufs=2))
+        psum = stack.enter_context(tc.psum_pool(name="psum", bufs=6))
+
+        gate_planes = keep.tile([P, 2, 2 * D], U8, align_bytes=64)
+        update_planes = keep.tile([P, 2, D], U8, align_bytes=64)
+        x_pad = keep.tile([P, P], BF16)
+        r_rows = keep.tile([P, UNITS], BF16)
+        nc.vector.memset(x_pad[:], 0.0)
+        nc.vector.memset(x_pad[:, ONES_ROW : ONES_ROW + 1], 1.0)
+        nc.vector.memset(r_rows[:].bitcast(I32), 0)
+        nc.vector.memset(gate_planes[:].rearrange("p g n -> p (g n)").bitcast(I32), 0)
+        nc.vector.memset(update_planes[:].rearrange("p g n -> p (g n)").bitcast(I32), 0)
+
+        ident_bf = keep.tile([P, P], BF16)
+        ident_f32 = keep.tile([P, P], F32)
+        make_identity(nc, ident_bf[:])
+        make_identity(nc, ident_f32[:])
+
+        hidden_sb = keep.tile([P, UNITS], BF16)
+        gate_words = keep.tile([P, N_VAR, 2 * D], U32, align_bytes=64)
+        update_words = keep.tile([P, N_VAR, D], U32, align_bytes=64)
+
+        def load_planes(planes, scales, half):
+            for quadrant in range(4):
+                nc.sync.dma_start(
+                    out=planes[32 * quadrant : 32 * quadrant + 16, half, :].bitcast(I32),
+                    in_=scales[HALF * half : HALF * (half + 1), 4 * quadrant : 4 * quadrant + 4, :].bitcast(I32),
+                )
+
+        def load_words(words_sb, words, v):
+            nc.sync.dma_start(out=words_sb[:, v, :].bitcast(I32), in_=words[v].rearrange("p n t -> p (n t)").bitcast(I32))
+
+        nc.sync.dma_start(out=hidden_sb[:], in_=hidden)
+        nc.sync.dma_start(out=x_pad[:, 0:N_VAR], in_=inputs)
+        for v in range(HALF, N_VAR):
+            nc.sync.dma_start(
+                out=r_rows[v : v + 1, 2 * D * (v - HALF) : 2 * D * (v - HALF + 1)],
+                in_=gate_w_I2H[v].rearrange("o c i -> o (c i)"),
+            )
+        nc.sync.dma_start(out=r_rows[ONES_ROW : ONES_ROW + 1, :], in_=gate_bias[UNITS : 2 * UNITS].rearrange("(o n) -> o n", o=1))
+        load_planes(gate_planes, gate_w_H2H_scales, 1)
+        for v in range(HALF, N_VAR):
+            load_words(gate_words, gate_w_H2H_words, v)
+        x_all = keep.tile([P, P, N_VAR], BF16)
+        nc.sync.dma_start(out=x_all[:].rearrange("c b v -> c (b v)"), in_=inputs.rearrange("b v -> (b v)").partition_broadcast(P))
+        small_rows = keep.tile([P, P], BF16)
+        nc.sync.dma_start(out=small_rows[0:32, :], in_=gate_w_I2H[0:HALF].rearrange("v o (m c) i -> (v o m) (c i)", c=P))
+        nc.sync.dma_start(out=small_rows[32:64, :], in_=gate_bias[0:UNITS].rearrange("(r c) -> r c", c=P))
+        nc.sync.dma_start(out=small_rows[64:96, :], in_=update_w_I2H.rearrange("v o (m c) i -> (v o m) (c i)", c=P))
+        nc.sync.dma_start(out=small_rows[96:P, :], in_=update_bias.rearrange("(r c) -> r c", c=P))
+        load_planes(gate_planes, gate_w_H2H_scales, 0)
+        load_planes(update_planes, update_w_H2H_scales, 0)
+        load_planes(update_planes, update_w_H2H_scales, 1)
+        for v in range(HALF):
+            load_words(gate_words, gate_w_H2H_words, v)
+        for v in range(N_VAR):
+            load_words(update_words, update_w_H2H_words, v)
+
+        x_t = psum_k.tile([P, P], BF16, tag="k")
+        nc.tensor.transpose(x_t[:], x_pad[:], ident_bf[:])
+        x_rows = keep.tile([P, P], BF16)
+        nc.scalar.copy(out=x_rows[:], in_=x_t[:])
+
+        def by_variable(units):
+            return units.rearrange("b (p t v) -> b v t p", t=PACK, v=N_VAR)
+
+        r_affine = keep.tile([P, N_VAR, PACK, P], F32)
+
+        def affine_bank(k):
+            affine_ps = psum.tile([P, BANK], F32, tag="bank")
+            nc.tensor.matmul(out=affine_ps[:], lhsT=x_rows[:], rhs=r_rows[:, BANK * k : BANK * (k + 1)], start=True, stop=True)
+            nc.scalar.copy(out=r_affine[:, :, :, P_PER_BANK * k : P_PER_BANK * (k + 1)], in_=by_variable(affine_ps[:]))
+
+        def h_to_k(pair):
+            k_first = psum_k.tile([P, 2, PACK, P], BF16, tag="k")
+            for i in range(2):
+                for t in range(PACK):
+                    nc.tensor.transpose(k_first[:, i, t, :], h_sorted[:, 2 * pair + i, t, :], ident_bf[:])
+            return k_first[:].rearrange("p i t b -> p i b t")
+
+        def quantise(grouped, first, count, codes, planes):
+            these = slice(first, first + count)
+            nc.vector.quantize_mx(
+                out=codes[:, these, :].rearrange("p v b -> p (v b)").bitcast(FP8X4),
+                scales=planes[:, these, :].rearrange("p v b -> p (v b)"),
+                in_=grouped[:, these, :, :].rearrange("p v b t -> p (v b t)"),
+            )
+
+        def gate_transposed(words, w_planes, v, first, codes, planes, wi, bias, first_chunk, func):
+            acc = psum.tile([P, CHUNKS, P], F32, tag="bank")
+            offset = 4 * (v % HALF)
+            for i in range(CHUNKS):
+                cols = slice(first + P * i, first + P * (i + 1))
+                nc.tensor.matmul_mx(
+                    out=acc[:, i, :],
+                    lhsT=words[:, v, cols].bitcast(FP8X4),
+                    lhsT_scale=w_planes[offset:P, v // HALF, cols],
+                    rhs=codes[:, v, :].bitcast(FP8X4),
+                    rhs_scale=planes[:, v, :],
+                    start=True,
+                    stop=True,
+                )
+            pre = work.tile([P, CHUNKS, P], F32)
+            gate_t = work.tile([P, CHUNKS, P], F32)
+            for i in range(CHUNKS):
+                chunk = first_chunk + i
+                nc.vector.scalar_tensor_tensor(
+                    out=pre[:, i, :],
+                    in0=x_all[:, :, v],
+                    scalar=wi[:, chunk : chunk + 1],
+                    in1=acc[:, i, :],
+                    op0=ALU.mult,
+                    op1=ALU.add,
+                )
+                nc.scalar.activation(out=gate_t[:, i, :], in_=pre[:, i, :], func=func, bias=bias[:, chunk : chunk + 1], scale=1.0)
+            return gate_t
+
+        def transposed_back(gate_t):
+            back = psum.tile([P, BANK], F32, tag="bank")
+            for i in range(CHUNKS):
+                nc.tensor.transpose(back[:, P * i : P * (i + 1)], gate_t[:, i, :], ident_f32[:])
+            return back
+
+        h_sorted = keep.tile([P, N_VAR, PACK, P], BF16)
+        h_grouped = keep.tile([P, N_VAR, P, PACK], BF16, align_bytes=64)
+        h_codes = keep.tile([P, N_VAR, P], U32, align_bytes=64)
+        h_planes = keep.tile([P, N_VAR, P], U8, align_bytes=64)
+        nc.vector.tensor_copy(out=h_sorted[:, 4:6], in_=by_variable(hidden_sb[:])[:, 4:6])
+        nc.vector.tensor_copy(out=h_sorted[:, 6:8], in_=by_variable(hidden_sb[:])[:, 6:8])
+        nc.gpsimd.tensor_scalar(out=h_sorted[:, 0:4], in0=by_variable(hidden_sb[:])[:, 0:4], scalar1=1.0, scalar2=0.0, op0=ALU.mult, op1=ALU.add)
+        for pair in (2, 3):
+            affine_bank(2 * pair - 4)
+            affine_bank(2 * pair - 3)
+            nc.vector.tensor_copy(out=h_grouped[:, 2 * pair : 2 * pair + 2], in_=h_to_k(pair))
+            quantise(h_grouped, 2 * pair, 2, h_codes, h_planes)
+        for k in range(HALF, N_BANKS):
+            affine_bank(k)
+
+        r_pre = keep.tile([P, N_VAR, PACK, P], F32)
+        r_sorted = keep.tile([P, N_VAR, PACK, P], F32)
+        for k in range(N_BANKS):
+            v = HALF + k // 2
+            cols = slice(BANK * (k % 2), BANK * (k % 2 + 1))
+            acc = psum.tile([P, BANK], F32, tag="bank")
+            nc.tensor.matmul_mx(
+                out=acc[:],
+                lhsT=h_codes[:, v, :].bitcast(FP8X4),
+                lhsT_scale=h_planes[:, v, :],
+                rhs=gate_words[:, v, cols].bitcast(FP8X4),
+                rhs_scale=gate_planes[4 * (v % HALF) : P, 1, cols],
+                start=True,
+                stop=True,
+            )
+            these = slice(P_PER_BANK * k, P_PER_BANK * (k + 1))
+            nc.vector.tensor_tensor(out=r_pre[:, :, :, these], in0=r_affine[:, :, :, these], in1=by_variable(acc[:]), op=ALU.add)
+            nc.scalar.activation(out=r_sorted[:, :, :, these], in_=r_pre[:, :, :, these], func=ACT.Sigmoid)
+            if k in (1, 3):
+                pair = k // 2
+                nc.scalar.copy(out=h_grouped[:, 2 * pair : 2 * pair + 2], in_=h_to_k(pair))
+        quantise(h_grouped, 0, HALF, h_codes, h_planes)
+
+        small_t = psum_k.tile([P, P], BF16, tag="k")
+        nc.tensor.transpose(small_t[:], small_rows[:], ident_bf[:])
+        columns = keep.tile([P, P], F32)
+        nc.vector.tensor_copy(out=columns[:], in_=small_t[:])
+        z_wi = columns[:, 0:32]
+        z_bias = columns[:, 32:64]
+        update_wi = columns[:, 64:96]
+        update_b = columns[:, 96:128]
+
+        hr_grouped = keep.tile([P, N_VAR, P, PACK], BF16, align_bytes=64)
+        hr_codes = keep.tile([P, N_VAR, P], U32, align_bytes=64)
+        hr_planes = keep.tile([P, N_VAR, P], U8, align_bytes=64)
+        zs = keep.tile([P, UNITS], F32)
+        kept = keep.tile([P, UNITS], F32)
+
+        def finish_z(k, z_t):
+            cols = slice(BANK * k, BANK * (k + 1))
+            back = transposed_back(z_t)
+            nc.scalar.copy(out=zs[:, cols], in_=back[:])
+            nc.gpsimd.tensor_tensor(out=kept[:, cols], in0=zs[:, cols], in1=hidden_sb[:, cols], op=ALU.mult)
+
+        def finish_out(v, g_t):
+            cols = slice(BANK * v, BANK * (v + 1))
+            back = transposed_back(g_t)
+            minus_new = work.tile([P, BANK], F32)
+            nc.vector.scalar_tensor_tensor(out=minus_new[:], in0=zs[:, cols], scalar=1.0, in1=back[:], op0=ALU.subtract, op1=ALU.mult)
+            result = work.tile([P, BANK], F32)
+            nc.gpsimd.tensor_tensor(out=result[:], in0=kept[:, cols], in1=minus_new[:], op=ALU.subtract)
+            nc.sync.dma_start(out=out[:, cols], in_=result[:])
+
+        started = {}
+        for step in range(2 * N_BANKS + DEPTH):
+            if step < N_BANKS:
+                started[step] = gate_transposed(gate_words, gate_planes, step // 2, BANK * (step % 2), h_codes, h_planes, z_wi, z_bias, CHUNKS * step, ACT.Sigmoid)
+            elif step < 2 * N_BANKS:
+                v = step - N_BANKS
+                started[step] = gate_transposed(update_words, update_planes, v, 0, hr_codes, hr_planes, update_wi, update_b, CHUNKS * v, ACT.Tanh)
+            due = step - DEPTH
+            if 0 <= due < N_VAR:
+                r_k = psum_k.tile([P, PACK, P], F32, tag="k")
+                for t in range(PACK):
+                    nc.tensor.transpose(r_k[:, t, :], r_sorted[:, due, t, :], ident_f32[:])
+                finish_z(due, started[due])
+                nc.vector.tensor_tensor(out=hr_grouped[:, due], in0=h_grouped[:, due], in1=r_k[:].rearrange("p t b -> p b t"), op=ALU.mult)
+                if due % HALF == HALF - 1:
+                    quantise(hr_grouped, due - HALF + 1, HALF, hr_codes, hr_planes)
+            elif due >= N_VAR:
+                finish_out(due - N_BANKS, started[due])

@@ -90,8 +90,6 @@ def tile_grucell_e_kernel(
         load_planes(gate_planes, gate_w_H2H_scales, 1)
         for v in range(HALF, N_VAR):
             load_words(gate_words, gate_w_H2H_words, v)
-        x_all = keep.tile([P, P, N_VAR], BF16)
-        nc.sync.dma_start(out=x_all[:].rearrange("c b v -> c (b v)"), in_=inputs.rearrange("b v -> (b v)").partition_broadcast(P))
         small_rows = keep.tile([P, P], BF16)
         nc.sync.dma_start(out=small_rows[0:32, :], in_=gate_w_I2H[0:HALF].rearrange("v o (m c) i -> (v o m) (c i)", c=P))
         nc.sync.dma_start(out=small_rows[32:64, :], in_=gate_bias[0:UNITS].rearrange("(r c) -> r c", c=P))
@@ -155,7 +153,7 @@ def tile_grucell_e_kernel(
                 chunk = first_chunk + i
                 nc.vector.scalar_tensor_tensor(
                     out=pre[:, i, :],
-                    in0=x_all[:, :, v],
+                    in0=x_all[:, v, :],
                     scalar=wi[:, chunk : chunk + 1],
                     in1=acc[:, i, :],
                     op0=ALU.mult,
@@ -216,6 +214,11 @@ def tile_grucell_e_kernel(
         z_bias = columns[:, 32:64]
         update_wi = columns[:, 64:96]
         update_b = columns[:, 96:128]
+        x_all_t = psum_k.tile([P, N_VAR, P], BF16, tag="k")
+        for v in range(N_VAR):
+            nc.tensor.transpose(x_all_t[:, v, :], x_pad[:, v : v + 1].to_broadcast([P, P]), ident_bf[:])
+        x_all = keep.tile([P, N_VAR, P], BF16)
+        nc.vector.tensor_copy(out=x_all[:], in_=x_all_t[:])
 
         hr_grouped = keep.tile([P, N_VAR, P, PACK], BF16, align_bytes=64)
         hr_codes = keep.tile([P, N_VAR, P], U32, align_bytes=64)

@@ -46,7 +46,7 @@ def tile_grucell_e_kernel(
     with ExitStack() as stack:
         stack.enter_context(tc.manual_schedule())
         keep = stack.enter_context(tc.tile_pool(name="keep", bufs=1))
-        work = stack.enter_context(tc.tile_pool(name="work", bufs=3))
+        work = stack.enter_context(tc.tile_pool(name="work", bufs=4))
         psum_k = stack.enter_context(tc.psum_pool(name="psum_k", bufs=2))
         psum = stack.enter_context(tc.psum_pool(name="psum", bufs=6))
 
@@ -79,7 +79,6 @@ def tile_grucell_e_kernel(
         def load_words(words_sb, words, v):
             nc.sync.dma_start(out=words_sb[:, v, :].bitcast(I32), in_=words[v].rearrange("p n t -> p (n t)").bitcast(I32))
 
-        nc.sync.dma_start(out=hidden_sb[:], in_=hidden)
         nc.sync.dma_start(out=x_pad[:, 0:N_VAR], in_=inputs)
         for v in range(HALF, N_VAR):
             nc.sync.dma_start(
@@ -87,6 +86,9 @@ def tile_grucell_e_kernel(
                 in_=gate_w_I2H[v].rearrange("o c i -> o (c i)"),
             )
         nc.sync.dma_start(out=r_rows[ONES_ROW : ONES_ROW + 1, :], in_=gate_bias[UNITS : 2 * UNITS].rearrange("(o n) -> o n", o=1))
+        for part in range(2):
+            cols = slice(UNITS // 2 * part, UNITS // 2 * (part + 1))
+            nc.sync.dma_start(out=hidden_sb[:, cols], in_=hidden[:, cols])
         load_planes(gate_planes, gate_w_H2H_scales, 1)
         for v in range(HALF, N_VAR):
             load_words(gate_words, gate_w_H2H_words, v)
@@ -96,10 +98,10 @@ def tile_grucell_e_kernel(
         nc.sync.dma_start(out=small_rows[64:96, :], in_=update_w_I2H.rearrange("v o (m c) i -> (v o m) (c i)", c=P))
         nc.sync.dma_start(out=small_rows[96:P, :], in_=update_bias.rearrange("(r c) -> r c", c=P))
         load_planes(gate_planes, gate_w_H2H_scales, 0)
-        load_planes(update_planes, update_w_H2H_scales, 0)
-        load_planes(update_planes, update_w_H2H_scales, 1)
         for v in range(HALF):
             load_words(gate_words, gate_w_H2H_words, v)
+        load_planes(update_planes, update_w_H2H_scales, 0)
+        load_planes(update_planes, update_w_H2H_scales, 1)
         for v in range(N_VAR):
             load_words(update_words, update_w_H2H_words, v)
 
@@ -172,16 +174,20 @@ def tile_grucell_e_kernel(
         h_grouped = keep.tile([P, N_VAR, P, PACK], BF16, align_bytes=64)
         h_codes = keep.tile([P, N_VAR, P], U32, align_bytes=64)
         h_planes = keep.tile([P, N_VAR, P], U8, align_bytes=64)
-        nc.vector.tensor_copy(out=h_sorted[:, 4:6], in_=by_variable(hidden_sb[:])[:, 4:6])
-        nc.vector.tensor_copy(out=h_sorted[:, 6:8], in_=by_variable(hidden_sb[:])[:, 6:8])
-        nc.gpsimd.tensor_scalar(out=h_sorted[:, 0:4], in0=by_variable(hidden_sb[:])[:, 0:4], scalar1=1.0, scalar2=0.0, op0=ALU.mult, op1=ALU.add)
+        for k in range(N_BANKS):
+            affine_bank(k)
+        for part in range(2):
+            cols = slice(UNITS // 2 * part, UNITS // 2 * (part + 1))
+            these = slice(P // 2 * part, P // 2 * (part + 1))
+            unsorted = by_variable(hidden_sb[:, cols])
+            nc.vector.tensor_copy(out=h_sorted[:, 4:6, :, these], in_=unsorted[:, 4:6])
+            nc.vector.tensor_copy(out=h_sorted[:, 6:8, :, these], in_=unsorted[:, 6:8])
+            nc.gpsimd.tensor_scalar(out=h_sorted[:, 0:4, :, these], in0=unsorted[:, 0:4], scalar1=1.0, scalar2=0.0, op0=ALU.mult, op1=ALU.add)
         for pair in (2, 3):
-            affine_bank(2 * pair - 4)
-            affine_bank(2 * pair - 3)
             nc.vector.tensor_copy(out=h_grouped[:, 2 * pair : 2 * pair + 2], in_=h_to_k(pair))
             quantise(h_grouped, 2 * pair, 2, h_codes, h_planes)
-        for k in range(HALF, N_BANKS):
-            affine_bank(k)
+        for pair in (0, 1):
+            nc.scalar.copy(out=h_grouped[:, 2 * pair : 2 * pair + 2], in_=h_to_k(pair))
 
         r_pre = keep.tile([P, N_VAR, PACK, P], F32)
         r_sorted = keep.tile([P, N_VAR, PACK, P], F32)
@@ -201,9 +207,6 @@ def tile_grucell_e_kernel(
             these = slice(P_PER_BANK * k, P_PER_BANK * (k + 1))
             nc.vector.tensor_tensor(out=r_pre[:, :, :, these], in0=r_affine[:, :, :, these], in1=by_variable(acc[:]), op=ALU.add)
             nc.scalar.activation(out=r_sorted[:, :, :, these], in_=r_pre[:, :, :, these], func=ACT.Sigmoid)
-            if k in (1, 3):
-                pair = k // 2
-                nc.scalar.copy(out=h_grouped[:, 2 * pair : 2 * pair + 2], in_=h_to_k(pair))
         quantise(h_grouped, 0, HALF, h_codes, h_planes)
 
         small_t = psum_k.tile([P, P], BF16, tag="k")
@@ -238,7 +241,8 @@ def tile_grucell_e_kernel(
             minus_new = work.tile([P, BANK], F32)
             nc.vector.scalar_tensor_tensor(out=minus_new[:], in0=zs[:, cols], scalar=1.0, in1=back[:], op0=ALU.subtract, op1=ALU.mult)
             result = work.tile([P, BANK], F32)
-            nc.gpsimd.tensor_tensor(out=result[:], in0=kept[:, cols], in1=minus_new[:], op=ALU.subtract)
+            last_step = nc.vector if v % 4 == 3 else nc.gpsimd
+            last_step.tensor_tensor(out=result[:], in0=kept[:, cols], in1=minus_new[:], op=ALU.subtract)
             nc.sync.dma_start(out=out[:, cols], in_=result[:])
 
         started = {}
@@ -248,14 +252,17 @@ def tile_grucell_e_kernel(
             elif step < 2 * N_BANKS:
                 v = step - N_BANKS
                 started[step] = gate_transposed(update_words, update_planes, v, 0, hr_codes, hr_planes, update_wi, update_b, CHUNKS * v, ACT.Tanh)
-            due = step - DEPTH
-            if 0 <= due < N_VAR:
+            turned = step - 1
+            if 0 <= turned < N_VAR:
                 r_k = psum_k.tile([P, PACK, P], F32, tag="k")
                 for t in range(PACK):
-                    nc.tensor.transpose(r_k[:, t, :], r_sorted[:, due, t, :], ident_f32[:])
+                    nc.tensor.transpose(r_k[:, t, :], r_sorted[:, turned, t, :], ident_f32[:])
+            due = step - DEPTH
+            if 0 <= due < N_BANKS:
                 finish_z(due, started[due])
-                nc.vector.tensor_tensor(out=hr_grouped[:, due], in0=h_grouped[:, due], in1=r_k[:].rearrange("p t b -> p b t"), op=ALU.mult)
-                if due % HALF == HALF - 1:
-                    quantise(hr_grouped, due - HALF + 1, HALF, hr_codes, hr_planes)
-            elif due >= N_VAR:
+            elif due >= N_BANKS:
                 finish_out(due - N_BANKS, started[due])
+            if 0 <= turned < N_VAR:
+                nc.vector.tensor_tensor(out=hr_grouped[:, turned], in0=h_grouped[:, turned], in1=r_k[:].rearrange("p t b -> p b t"), op=ALU.mult)
+                if turned % HALF == HALF - 1:
+                    quantise(hr_grouped, turned - HALF + 1, HALF, hr_codes, hr_planes)

@@ -79,6 +79,7 @@ def tile_grucell_e_kernel(
         def load_words(words_sb, words, v):
             nc.sync.dma_start(out=words_sb[:, v, :].bitcast(I32), in_=words[v].rearrange("p n t -> p (n t)").bitcast(I32))
 
+        nc.sync.dma_start(out=hidden_sb[:], in_=hidden)
         nc.sync.dma_start(out=x_pad[:, 0:N_VAR], in_=inputs)
         for v in range(HALF, N_VAR):
             nc.sync.dma_start(
@@ -86,9 +87,6 @@ def tile_grucell_e_kernel(
                 in_=gate_w_I2H[v].rearrange("o c i -> o (c i)"),
             )
         nc.sync.dma_start(out=r_rows[ONES_ROW : ONES_ROW + 1, :], in_=gate_bias[UNITS : 2 * UNITS].rearrange("(o n) -> o n", o=1))
-        for part in range(2):
-            cols = slice(UNITS // 2 * part, UNITS // 2 * (part + 1))
-            nc.sync.dma_start(out=hidden_sb[:, cols], in_=hidden[:, cols])
         load_planes(gate_planes, gate_w_H2H_scales, 1)
         for v in range(HALF, N_VAR):
             load_words(gate_words, gate_w_H2H_words, v)
@@ -98,10 +96,10 @@ def tile_grucell_e_kernel(
         nc.sync.dma_start(out=small_rows[64:96, :], in_=update_w_I2H.rearrange("v o (m c) i -> (v o m) (c i)", c=P))
         nc.sync.dma_start(out=small_rows[96:P, :], in_=update_bias.rearrange("(r c) -> r c", c=P))
         load_planes(gate_planes, gate_w_H2H_scales, 0)
-        for v in range(HALF):
-            load_words(gate_words, gate_w_H2H_words, v)
         load_planes(update_planes, update_w_H2H_scales, 0)
         load_planes(update_planes, update_w_H2H_scales, 1)
+        for v in range(HALF):
+            load_words(gate_words, gate_w_H2H_words, v)
         for v in range(N_VAR):
             load_words(update_words, update_w_H2H_words, v)
 
@@ -174,20 +172,16 @@ def tile_grucell_e_kernel(
         h_grouped = keep.tile([P, N_VAR, P, PACK], BF16, align_bytes=64)
         h_codes = keep.tile([P, N_VAR, P], U32, align_bytes=64)
         h_planes = keep.tile([P, N_VAR, P], U8, align_bytes=64)
-        for k in range(N_BANKS):
-            affine_bank(k)
-        for part in range(2):
-            cols = slice(UNITS // 2 * part, UNITS // 2 * (part + 1))
-            these = slice(P // 2 * part, P // 2 * (part + 1))
-            unsorted = by_variable(hidden_sb[:, cols])
-            nc.vector.tensor_copy(out=h_sorted[:, 4:6, :, these], in_=unsorted[:, 4:6])
-            nc.vector.tensor_copy(out=h_sorted[:, 6:8, :, these], in_=unsorted[:, 6:8])
-            nc.gpsimd.tensor_scalar(out=h_sorted[:, 0:4, :, these], in0=unsorted[:, 0:4], scalar1=1.0, scalar2=0.0, op0=ALU.mult, op1=ALU.add)
+        nc.vector.tensor_copy(out=h_sorted[:, 4:6], in_=by_variable(hidden_sb[:])[:, 4:6])
+        nc.vector.tensor_copy(out=h_sorted[:, 6:8], in_=by_variable(hidden_sb[:])[:, 6:8])
+        nc.gpsimd.tensor_scalar(out=h_sorted[:, 0:4], in0=by_variable(hidden_sb[:])[:, 0:4], scalar1=1.0, scalar2=0.0, op0=ALU.mult, op1=ALU.add)
         for pair in (2, 3):
+            affine_bank(2 * pair - 4)
+            affine_bank(2 * pair - 3)
             nc.vector.tensor_copy(out=h_grouped[:, 2 * pair : 2 * pair + 2], in_=h_to_k(pair))
             quantise(h_grouped, 2 * pair, 2, h_codes, h_planes)
-        for pair in (0, 1):
-            nc.scalar.copy(out=h_grouped[:, 2 * pair : 2 * pair + 2], in_=h_to_k(pair))
+        for k in range(HALF, N_BANKS):
+            affine_bank(k)
 
         r_pre = keep.tile([P, N_VAR, PACK, P], F32)
         r_sorted = keep.tile([P, N_VAR, PACK, P], F32)
@@ -207,6 +201,9 @@ def tile_grucell_e_kernel(
             these = slice(P_PER_BANK * k, P_PER_BANK * (k + 1))
             nc.vector.tensor_tensor(out=r_pre[:, :, :, these], in0=r_affine[:, :, :, these], in1=by_variable(acc[:]), op=ALU.add)
             nc.scalar.activation(out=r_sorted[:, :, :, these], in_=r_pre[:, :, :, these], func=ACT.Sigmoid)
+            if k in (1, 3):
+                pair = k // 2
+                nc.scalar.copy(out=h_grouped[:, 2 * pair : 2 * pair + 2], in_=h_to_k(pair))
         quantise(h_grouped, 0, HALF, h_codes, h_planes)
 
         small_t = psum_k.tile([P, P], BF16, tag="k")

@@ -118,12 +118,13 @@ def tile_grucell_e_kernel(
             nc.tensor.matmul(out=affine_ps[:], lhsT=x_rows[:], rhs=r_rows[:, BANK * k : BANK * (k + 1)], start=True, stop=True)
             nc.scalar.copy(out=r_affine[:, :, :, P_PER_BANK * k : P_PER_BANK * (k + 1)], in_=by_variable(affine_ps[:]))
 
+        h_words = hidden_sb[:].bitcast(F32).rearrange("b (p t w) -> b w t p", t=PACK, w=N_VAR // 2)
+
         def h_to_k(pair):
-            k_first = psum_k.tile([P, 2, PACK, P], BF16, tag="k")
-            for i in range(2):
-                for t in range(PACK):
-                    nc.tensor.transpose(k_first[:, i, t, :], h_sorted[:, 2 * pair + i, t, :], ident_bf[:])
-            return k_first[:].rearrange("p i t b -> p i b t")
+            k_first = psum_k.tile([P, PACK, P], F32, tag="k")
+            for t in range(PACK):
+                nc.tensor.transpose(k_first[:, t, :], h_words[:, pair, t, :], ident_f32[:])
+            return k_first[:].bitcast(BF16).rearrange("p t (b i) -> p i b t", i=2)
 
         def quantise(grouped, first, count, codes, planes):
             these = slice(first, first + count)
@@ -148,7 +149,8 @@ def tile_grucell_e_kernel(
                     stop=True,
                 )
             pre = work.tile([P, CHUNKS, P], F32)
-            gate_t = work.tile([P, CHUNKS, P], F32)
+            if func is not None:
+                gate_t = work.tile([P, CHUNKS, P], F32)
             for i in range(CHUNKS):
                 chunk = first_chunk + i
                 nc.vector.scalar_tensor_tensor(
@@ -159,8 +161,9 @@ def tile_grucell_e_kernel(
                     op0=ALU.mult,
                     op1=ALU.add,
                 )
-                nc.scalar.activation(out=gate_t[:, i, :], in_=pre[:, i, :], func=func, bias=bias[:, chunk : chunk + 1], scale=1.0)
-            return gate_t
+                if func is not None:
+                    nc.scalar.activation(out=gate_t[:, i, :], in_=pre[:, i, :], func=func, bias=bias[:, chunk : chunk + 1], scale=1.0)
+            return pre if func is None else gate_t
 
         def transposed_back(gate_t):
             back = psum.tile([P, BANK], F32, tag="bank")
@@ -168,13 +171,9 @@ def tile_grucell_e_kernel(
                 nc.tensor.transpose(back[:, P * i : P * (i + 1)], gate_t[:, i, :], ident_f32[:])
             return back
 
-        h_sorted = keep.tile([P, N_VAR, PACK, P], BF16)
         h_grouped = keep.tile([P, N_VAR, P, PACK], BF16, align_bytes=64)
         h_codes = keep.tile([P, N_VAR, P], U32, align_bytes=64)
         h_planes = keep.tile([P, N_VAR, P], U8, align_bytes=64)
-        nc.vector.tensor_copy(out=h_sorted[:, 4:6], in_=by_variable(hidden_sb[:])[:, 4:6])
-        nc.vector.tensor_copy(out=h_sorted[:, 6:8], in_=by_variable(hidden_sb[:])[:, 6:8])
-        nc.gpsimd.tensor_scalar(out=h_sorted[:, 0:4], in0=by_variable(hidden_sb[:])[:, 0:4], scalar1=1.0, scalar2=0.0, op0=ALU.mult, op1=ALU.add)
         for pair in (2, 3):
             affine_bank(2 * pair - 4)
             affine_bank(2 * pair - 3)
@@ -228,8 +227,12 @@ def tile_grucell_e_kernel(
 
         def finish_z(k, z_t):
             cols = slice(BANK * k, BANK * (k + 1))
-            back = transposed_back(z_t)
-            nc.scalar.copy(out=zs[:, cols], in_=back[:])
+            back = psum.tile([P, BANK], F32, tag="bank")
+            for i in range(CHUNKS):
+                bias_column = z_bias[:, CHUNKS * k + i : CHUNKS * k + i + 1].to_broadcast([P, P])
+                nc.tensor.matmul(out=back[:, P * i : P * (i + 1)], lhsT=bias_column, rhs=ident_f32[:], is_transpose=True, start=True, stop=False)
+                nc.tensor.matmul(out=back[:, P * i : P * (i + 1)], lhsT=z_t[:, i, :], rhs=ident_f32[:], is_transpose=True, start=False, stop=True)
+            nc.scalar.activation(out=zs[:, cols], in_=back[:], func=ACT.Sigmoid)
             nc.gpsimd.tensor_tensor(out=kept[:, cols], in0=zs[:, cols], in1=hidden_sb[:, cols], op=ALU.mult)
 
         def finish_out(v, g_t):
@@ -245,7 +248,7 @@ def tile_grucell_e_kernel(
         started = {}
         for step in range(2 * N_BANKS + DEPTH):
             if step < N_BANKS:
-                started[step] = gate_transposed(gate_words, gate_planes, step // 2, BANK * (step % 2), h_codes, h_planes, z_wi, z_bias, CHUNKS * step, ACT.Sigmoid)
+                started[step] = gate_transposed(gate_words, gate_planes, step // 2, BANK * (step % 2), h_codes, h_planes, z_wi, z_bias, CHUNKS * step, None)
             elif step < 2 * N_BANKS:
                 v = step - N_BANKS
                 started[step] = gate_transposed(update_words, update_planes, v, 0, hr_codes, hr_planes, update_wi, update_b, CHUNKS * v, ACT.Tanh)

@@ -21,9 +21,9 @@ BANK = 512
 N_BANKS = UNITS // BANK
 CHUNKS = BANK // P
 HALF = N_VAR // 2
+LAG = 3
 P_PER_BANK = BANK // (PACK * N_VAR)
 ONES_ROW = 16
-DEPTH = 2
 
 FLOPS = 2 * P * D * (3 * D) * N_VAR
 
@@ -53,17 +53,25 @@ def tile_grucell_e_kernel(
         gate_planes = keep.tile([P, 2, 2 * D], U8, align_bytes=64)
         update_planes = keep.tile([P, 2, D], U8, align_bytes=64)
         x_pad = keep.tile([P, P], BF16)
-        r_rows = keep.tile([P, UNITS], BF16)
+        z_rows = keep.tile([P, 2 * D], BF16)
+        r_small = keep.tile([P, P], BF16)
         nc.vector.memset(x_pad[:], 0.0)
-        nc.vector.memset(x_pad[:, ONES_ROW : ONES_ROW + 1], 1.0)
-        nc.vector.memset(r_rows[:].bitcast(I32), 0)
+        nc.vector.memset(r_small[:].bitcast(I32), 0)
+        nc.vector.memset(x_pad[:, ONES_ROW : ONES_ROW + HALF], 1.0)
         nc.vector.memset(gate_planes[:].rearrange("p g n -> p (g n)").bitcast(I32), 0)
         nc.vector.memset(update_planes[:].rearrange("p g n -> p (g n)").bitcast(I32), 0)
+        nc.vector.memset(z_rows[:].bitcast(I32), 0)
+        nc.scalar.dma_start(out=x_pad[:, 0:N_VAR], in_=inputs)
+        nc.scalar.dma_start(out=r_small[0:32, :], in_=gate_w_I2H[HALF:N_VAR].rearrange("v o (m c) i -> (v o m) (c i)", c=P))
+        nc.scalar.dma_start(out=r_small[32:64, :], in_=gate_bias[UNITS : 2 * UNITS].rearrange("(r c) -> r c", c=P))
+        warm = keep.tile([P, 1], F32)
+        nc.gpsimd.memset(warm[:], 0.0)
+        nc.scalar.activation(out=warm[:], in_=warm[:], func=ACT.Sigmoid)
 
-        ident_bf = keep.tile([P, P], BF16)
         ident_f32 = keep.tile([P, P], F32)
-        make_identity(nc, ident_bf[:])
         make_identity(nc, ident_f32[:])
+        ident_bf = keep.tile([P, P], BF16)
+        nc.vector.tensor_copy(out=ident_bf[:], in_=ident_f32[:])
 
         hidden_sb = keep.tile([P, UNITS], BF16)
         gate_words = keep.tile([P, N_VAR, 2 * D], U32, align_bytes=64)
@@ -80,43 +88,25 @@ def tile_grucell_e_kernel(
             nc.sync.dma_start(out=words_sb[:, v, :].bitcast(I32), in_=words[v].rearrange("p n t -> p (n t)").bitcast(I32))
 
         nc.sync.dma_start(out=hidden_sb[:], in_=hidden)
-        nc.sync.dma_start(out=x_pad[:, 0:N_VAR], in_=inputs)
-        for v in range(HALF, N_VAR):
-            nc.sync.dma_start(
-                out=r_rows[v : v + 1, 2 * D * (v - HALF) : 2 * D * (v - HALF + 1)],
-                in_=gate_w_I2H[v].rearrange("o c i -> o (c i)"),
-            )
-        nc.sync.dma_start(out=r_rows[ONES_ROW : ONES_ROW + 1, :], in_=gate_bias[UNITS : 2 * UNITS].rearrange("(o n) -> o n", o=1))
         load_planes(gate_planes, gate_w_H2H_scales, 1)
         for v in range(HALF, N_VAR):
             load_words(gate_words, gate_w_H2H_words, v)
-        small_rows = keep.tile([P, P], BF16)
-        nc.sync.dma_start(out=small_rows[0:32, :], in_=gate_w_I2H[0:HALF].rearrange("v o (m c) i -> (v o m) (c i)", c=P))
-        nc.sync.dma_start(out=small_rows[32:64, :], in_=gate_bias[0:UNITS].rearrange("(r c) -> r c", c=P))
-        nc.sync.dma_start(out=small_rows[64:96, :], in_=update_w_I2H.rearrange("v o (m c) i -> (v o m) (c i)", c=P))
-        nc.sync.dma_start(out=small_rows[96:P, :], in_=update_bias.rearrange("(r c) -> r c", c=P))
+        u_small = keep.tile([P, P], BF16)
+        nc.vector.memset(u_small[:].bitcast(I32), 0)
+        nc.gpsimd.dma_start(out=z_rows[0:HALF, :], in_=gate_w_I2H[0:HALF].rearrange("v o c i -> v (o c i)"))
+        nc.gpsimd.dma_start(out=z_rows[ONES_ROW : ONES_ROW + HALF, :], in_=gate_bias[0:UNITS].rearrange("(r c) -> r c", r=HALF))
+        nc.gpsimd.dma_start(out=u_small[0:32, :], in_=update_w_I2H.rearrange("v o (m c) i -> (v o m) (c i)", c=P))
+        nc.gpsimd.dma_start(out=u_small[32:64, :], in_=update_bias.rearrange("(r c) -> r c", c=P))
         load_planes(gate_planes, gate_w_H2H_scales, 0)
-        load_planes(update_planes, update_w_H2H_scales, 0)
-        load_planes(update_planes, update_w_H2H_scales, 1)
         for v in range(HALF):
             load_words(gate_words, gate_w_H2H_words, v)
+        load_planes(update_planes, update_w_H2H_scales, 0)
+        load_planes(update_planes, update_w_H2H_scales, 1)
         for v in range(N_VAR):
             load_words(update_words, update_w_H2H_words, v)
 
-        x_t = psum_k.tile([P, P], BF16, tag="k")
-        nc.tensor.transpose(x_t[:], x_pad[:], ident_bf[:])
-        x_rows = keep.tile([P, P], BF16)
-        nc.scalar.copy(out=x_rows[:], in_=x_t[:])
-
         def by_variable(units):
             return units.rearrange("b (p t v) -> b v t p", t=PACK, v=N_VAR)
-
-        r_affine = keep.tile([P, N_VAR, PACK, P], F32)
-
-        def affine_bank(k):
-            affine_ps = psum.tile([P, BANK], F32, tag="bank")
-            nc.tensor.matmul(out=affine_ps[:], lhsT=x_rows[:], rhs=r_rows[:, BANK * k : BANK * (k + 1)], start=True, stop=True)
-            nc.scalar.copy(out=r_affine[:, :, :, P_PER_BANK * k : P_PER_BANK * (k + 1)], in_=by_variable(affine_ps[:]))
 
         h_words = hidden_sb[:].bitcast(F32).rearrange("b (p t w) -> b w t p", t=PACK, w=N_VAR // 2)
 
@@ -134,7 +124,7 @@ def tile_grucell_e_kernel(
                 in_=grouped[:, these, :, :].rearrange("p v b t -> p (v b t)"),
             )
 
-        def gate_transposed(words, w_planes, v, first, codes, planes, wi, bias, first_chunk, func):
+        def product_transposed(words, w_planes, v, first, codes, planes):
             acc = psum.tile([P, CHUNKS, P], F32, tag="bank")
             offset = 4 * (v % HALF)
             for i in range(CHUNKS):
@@ -148,22 +138,7 @@ def tile_grucell_e_kernel(
                     start=True,
                     stop=True,
                 )
-            pre = work.tile([P, CHUNKS, P], F32)
-            if func is not None:
-                gate_t = work.tile([P, CHUNKS, P], F32)
-            for i in range(CHUNKS):
-                chunk = first_chunk + i
-                nc.vector.scalar_tensor_tensor(
-                    out=pre[:, i, :],
-                    in0=x_all[:, v, :],
-                    scalar=wi[:, chunk : chunk + 1],
-                    in1=acc[:, i, :],
-                    op0=ALU.mult,
-                    op1=ALU.add,
-                )
-                if func is not None:
-                    nc.scalar.activation(out=gate_t[:, i, :], in_=pre[:, i, :], func=func, bias=bias[:, chunk : chunk + 1], scale=1.0)
-            return pre if func is None else gate_t
+            return acc
 
         def transposed_back(gate_t):
             back = psum.tile([P, BANK], F32, tag="bank")
@@ -171,53 +146,78 @@ def tile_grucell_e_kernel(
                 nc.tensor.transpose(back[:, P * i : P * (i + 1)], gate_t[:, i, :], ident_f32[:])
             return back
 
-        h_grouped = keep.tile([P, N_VAR, P, PACK], BF16, align_bytes=64)
-        h_codes = keep.tile([P, N_VAR, P], U32, align_bytes=64)
-        h_planes = keep.tile([P, N_VAR, P], U8, align_bytes=64)
-        for pair in (2, 3):
-            affine_bank(2 * pair - 4)
-            affine_bank(2 * pair - 3)
-            nc.vector.tensor_copy(out=h_grouped[:, 2 * pair : 2 * pair + 2], in_=h_to_k(pair))
-            quantise(h_grouped, 2 * pair, 2, h_codes, h_planes)
-        for k in range(HALF, N_BANKS):
-            affine_bank(k)
+        def columns_of(small, name):
+            turned = psum_k.tile([P, P], BF16, tag="k")
+            nc.tensor.transpose(turned[:], small[:], ident_bf[:])
+            columns = keep.tile([P, 64], F32, name=name)
+            nc.vector.tensor_copy(out=columns[:], in_=turned[:, 0:64])
+            return columns
 
-        r_pre = keep.tile([P, N_VAR, PACK, P], F32)
-        r_sorted = keep.tile([P, N_VAR, PACK, P], F32)
-        for k in range(N_BANKS):
-            v = HALF + k // 2
-            cols = slice(BANK * (k % 2), BANK * (k % 2 + 1))
-            acc = psum.tile([P, BANK], F32, tag="bank")
-            nc.tensor.matmul_mx(
-                out=acc[:],
-                lhsT=h_codes[:, v, :].bitcast(FP8X4),
-                lhsT_scale=h_planes[:, v, :],
-                rhs=gate_words[:, v, cols].bitcast(FP8X4),
-                rhs_scale=gate_planes[4 * (v % HALF) : P, 1, cols],
-                start=True,
-                stop=True,
-            )
-            these = slice(P_PER_BANK * k, P_PER_BANK * (k + 1))
-            nc.vector.tensor_tensor(out=r_pre[:, :, :, these], in0=r_affine[:, :, :, these], in1=by_variable(acc[:]), op=ALU.add)
-            nc.scalar.activation(out=r_sorted[:, :, :, these], in_=r_pre[:, :, :, these], func=ACT.Sigmoid)
-            if k in (1, 3):
-                pair = k // 2
-                nc.scalar.copy(out=h_grouped[:, 2 * pair : 2 * pair + 2], in_=h_to_k(pair))
-        quantise(h_grouped, 0, HALF, h_codes, h_planes)
-
-        small_t = psum_k.tile([P, P], BF16, tag="k")
-        nc.tensor.transpose(small_t[:], small_rows[:], ident_bf[:])
-        columns = keep.tile([P, P], F32)
-        nc.vector.tensor_copy(out=columns[:], in_=small_t[:])
-        z_wi = columns[:, 0:32]
-        z_bias = columns[:, 32:64]
-        update_wi = columns[:, 64:96]
-        update_b = columns[:, 96:128]
         x_all_t = psum_k.tile([P, N_VAR, P], BF16, tag="k")
         for v in range(N_VAR):
             nc.tensor.transpose(x_all_t[:, v, :], x_pad[:, v : v + 1].to_broadcast([P, P]), ident_bf[:])
         x_all = keep.tile([P, N_VAR, P], BF16)
-        nc.vector.tensor_copy(out=x_all[:], in_=x_all_t[:])
+        nc.scalar.copy(out=x_all[:], in_=x_all_t[:])
+        mask = keep.tile([P, HALF], F32)
+        nc.vector.tensor_tensor(out=mask[:], in0=ident_f32[:, 0:HALF], in1=ident_f32[:, ONES_ROW : ONES_ROW + HALF], op=ALU.add)
+        x_t = psum.tile([P, P], BF16, tag="bank")
+        nc.tensor.transpose(x_t[:], x_pad[:], ident_bf[:])
+        x_rows = keep.tile([P, HALF, P], BF16)
+        for v in range(HALF):
+            nc.vector.tensor_scalar(out=x_rows[:, v, :], in0=x_t[:], scalar1=mask[:, v : v + 1], scalar2=None, op0=ALU.mult)
+        r_columns = columns_of(r_small, "r_columns")
+
+        h_grouped = keep.tile([P, N_VAR, P, PACK], BF16, align_bytes=64)
+        h_codes = keep.tile([P, N_VAR, P], U32, align_bytes=64)
+        h_planes = keep.tile([P, N_VAR, P], U8, align_bytes=64)
+        r_sorted = keep.tile([P, N_VAR, PACK, P], F32)
+
+        def with_inputs(acc, v, wi, first_chunk):
+            pre = work.tile([P, CHUNKS, P], F32)
+            for i in range(CHUNKS):
+                scalar = wi[:, first_chunk + i : first_chunk + i + 1]
+                nc.vector.scalar_tensor_tensor(out=pre[:, i, :], in0=x_all[:, v, :], scalar=scalar, in1=acc[:, i, :], op0=ALU.mult, op1=ALU.add)
+            return pre
+
+        def start_r(k):
+            acc = product_transposed(gate_words, gate_planes, HALF + k // 2, BANK * (k % 2), h_codes, h_planes)
+            return with_inputs(acc, HALF + k // 2, r_columns, CHUNKS * k)
+
+        def finish_r(k, pre):
+            bank = psum.tile([P, BANK], F32, tag="bank")
+            for i in range(CHUNKS):
+                chunk = bank[:, P * i : P * (i + 1)]
+                bias = r_columns[:, 32 + CHUNKS * k + i : 33 + CHUNKS * k + i]
+                nc.tensor.matmul(out=chunk, lhsT=bias.to_broadcast([P, P]), rhs=ident_f32[:], is_transpose=True, start=True, stop=False)
+                nc.tensor.matmul(out=chunk, lhsT=pre[:, i, :], rhs=ident_f32[:], is_transpose=True, start=False, stop=True)
+            these = slice(P_PER_BANK * k, P_PER_BANK * (k + 1))
+            nc.scalar.activation(out=r_sorted[:, :, :, these], in_=by_variable(bank[:]), func=ACT.Sigmoid)
+
+        second = h_to_k(2)
+        third = h_to_k(3)
+        nc.vector.tensor_copy(out=h_grouped[:, 4:6], in_=second)
+        nc.scalar.copy(out=h_grouped[:, 6:8], in_=third)
+        quantise(h_grouped, 4, 2, h_codes, h_planes)
+        r_started = {}
+        for pair in range(5):
+            if pair < 4:
+                r_started[2 * pair] = start_r(2 * pair)
+                r_started[2 * pair + 1] = start_r(2 * pair + 1)
+            if pair == 0:
+                quantise(h_grouped, 6, 2, h_codes, h_planes)
+            if pair == 3:
+                nc.vector.tensor_copy(out=h_grouped[:, 2:4], in_=first)
+                quantise(h_grouped, 0, 2, h_codes, h_planes)
+                u_columns = columns_of(u_small, "u_columns")
+            if pair > 0:
+                finish_r(2 * pair - 2, r_started[2 * pair - 2])
+                finish_r(2 * pair - 1, r_started[2 * pair - 1])
+            if pair == 1:
+                zeroth = h_to_k(0)
+                nc.scalar.copy(out=h_grouped[:, 0:2], in_=zeroth)
+            if pair == 2:
+                first = h_to_k(1)
+        quantise(h_grouped, 2, 2, h_codes, h_planes)
 
         hr_grouped = keep.tile([P, N_VAR, P, PACK], BF16, align_bytes=64)
         hr_codes = keep.tile([P, N_VAR, P], U32, align_bytes=64)
@@ -225,15 +225,33 @@ def tile_grucell_e_kernel(
         zs = keep.tile([P, UNITS], F32)
         kept = keep.tile([P, UNITS], F32)
 
-        def finish_z(k, z_t):
+        def start_z(k):
+            acc = product_transposed(gate_words, gate_planes, k // 2, BANK * (k % 2), h_codes, h_planes)
+            z_t = work.tile([P, CHUNKS, P], F32)
+            nc.scalar.copy(out=z_t[:], in_=acc[:])
+            return z_t
+
+        def open_z(k):
+            bank = psum.tile([P, BANK], F32, tag="bank")
+            nc.tensor.matmul(out=bank[:], lhsT=x_rows[:, k // 2, :], rhs=z_rows[:, BANK * (k % 2) : BANK * (k % 2 + 1)], start=True, stop=False)
+            return bank
+
+        def finish_z(k, z_t, bank):
             cols = slice(BANK * k, BANK * (k + 1))
-            back = psum.tile([P, BANK], F32, tag="bank")
             for i in range(CHUNKS):
-                bias_column = z_bias[:, CHUNKS * k + i : CHUNKS * k + i + 1].to_broadcast([P, P])
-                nc.tensor.matmul(out=back[:, P * i : P * (i + 1)], lhsT=bias_column, rhs=ident_f32[:], is_transpose=True, start=True, stop=False)
-                nc.tensor.matmul(out=back[:, P * i : P * (i + 1)], lhsT=z_t[:, i, :], rhs=ident_f32[:], is_transpose=True, start=False, stop=True)
-            nc.scalar.activation(out=zs[:, cols], in_=back[:], func=ACT.Sigmoid)
+                chunk = bank[:, P * i : P * (i + 1)]
+                nc.tensor.matmul(out=chunk, lhsT=z_t[:, i, :], rhs=ident_f32[:], is_transpose=True, start=False, stop=i == CHUNKS - 1)
+            nc.scalar.activation(out=zs[:, cols], in_=bank[:], func=ACT.Sigmoid)
             nc.gpsimd.tensor_tensor(out=kept[:, cols], in0=zs[:, cols], in1=hidden_sb[:, cols], op=ALU.mult)
+
+        def start_out(v):
+            acc = product_transposed(update_words, update_planes, v, 0, hr_codes, hr_planes)
+            pre = with_inputs(acc, v, u_columns, CHUNKS * v)
+            g_t = work.tile([P, CHUNKS, P], F32)
+            for i in range(CHUNKS):
+                bias = u_columns[:, 32 + CHUNKS * v + i : 33 + CHUNKS * v + i]
+                nc.scalar.activation(out=g_t[:, i, :], in_=pre[:, i, :], func=ACT.Tanh, bias=bias, scale=1.0)
+            return g_t
 
         def finish_out(v, g_t):
             cols = slice(BANK * v, BANK * (v + 1))
@@ -241,28 +259,34 @@ def tile_grucell_e_kernel(
             minus_new = work.tile([P, BANK], F32)
             nc.vector.scalar_tensor_tensor(out=minus_new[:], in0=zs[:, cols], scalar=1.0, in1=back[:], op0=ALU.subtract, op1=ALU.mult)
             result = work.tile([P, BANK], F32)
-            last_step = nc.vector if v % 4 == 3 else nc.gpsimd
+            last_step = nc.vector if v in (3, 6, 7) else nc.gpsimd
             last_step.tensor_tensor(out=result[:], in0=kept[:, cols], in1=minus_new[:], op=ALU.subtract)
             nc.sync.dma_start(out=out[:, cols], in_=result[:])
 
-        started = {}
-        for step in range(2 * N_BANKS + DEPTH):
-            if step < N_BANKS:
-                started[step] = gate_transposed(gate_words, gate_planes, step // 2, BANK * (step % 2), h_codes, h_planes, z_wi, z_bias, CHUNKS * step, None)
-            elif step < 2 * N_BANKS:
-                v = step - N_BANKS
-                started[step] = gate_transposed(update_words, update_planes, v, 0, hr_codes, hr_planes, update_wi, update_b, CHUNKS * v, ACT.Tanh)
-            turned = step - 1
-            if 0 <= turned < N_VAR:
-                r_k = psum_k.tile([P, PACK, P], F32, tag="k")
-                for t in range(PACK):
-                    nc.tensor.transpose(r_k[:, t, :], r_sorted[:, turned, t, :], ident_f32[:])
-            due = step - DEPTH
-            if 0 <= due < N_BANKS:
-                finish_z(due, started[due])
-            elif due >= N_BANKS:
-                finish_out(due - N_BANKS, started[due])
-            if 0 <= turned < N_VAR:
-                nc.vector.tensor_tensor(out=hr_grouped[:, turned], in0=h_grouped[:, turned], in1=r_k[:].rearrange("p t b -> p b t"), op=ALU.mult)
-                if turned % HALF == HALF - 1:
-                    quantise(hr_grouped, turned - HALF + 1, HALF, hr_codes, hr_planes)
+        def turn_r(v):
+            r_k = psum_k.tile([P, PACK, P], F32, tag="k")
+            for t in range(PACK):
+                nc.tensor.transpose(r_k[:, t, :], r_sorted[:, v, t, :], ident_f32[:])
+            return r_k
+
+        def multiply_r(v, r_k):
+            nc.vector.tensor_tensor(out=hr_grouped[:, v], in0=h_grouped[:, v], in1=r_k[:].rearrange("p t b -> p b t"), op=ALU.mult)
+
+        z_started = {}
+        out_started = {}
+        for step in range(N_VAR + LAG + 1):
+            if 0 <= step < N_BANKS:
+                z_started[step] = start_z(step)
+            if 0 <= step - LAG < N_VAR:
+                out_started[step - LAG] = start_out(step - LAG)
+            if 0 <= step - 1 < N_BANKS:
+                z_bank = open_z(step - 1)
+            if step < N_VAR:
+                r_k = turn_r(step)
+                multiply_r(step, r_k)
+                if step % 2 == 1:
+                    quantise(hr_grouped, step - 1, 2, hr_codes, hr_planes)
+            if 0 <= step - 1 < N_BANKS:
+                finish_z(step - 1, z_started[step - 1], z_bank)
+            if 0 <= step - LAG - 1 < N_VAR:
+                finish_out(step - LAG - 1, out_started[step - LAG - 1])

@@ -61,9 +61,6 @@ def tile_grucell_e_kernel(
         nc.vector.memset(gate_planes[:].rearrange("p g n -> p (g n)").bitcast(I32), 0)
         nc.vector.memset(update_planes[:].rearrange("p g n -> p (g n)").bitcast(I32), 0)
         nc.vector.memset(z_rows[:].bitcast(I32), 0)
-        nc.scalar.dma_start(out=x_pad[:, 0:N_VAR], in_=inputs)
-        nc.scalar.dma_start(out=r_small[0:32, :], in_=gate_w_I2H[HALF:N_VAR].rearrange("v o (m c) i -> (v o m) (c i)", c=P))
-        nc.scalar.dma_start(out=r_small[32:64, :], in_=gate_bias[UNITS : 2 * UNITS].rearrange("(r c) -> r c", c=P))
         warm = keep.tile([P, 1], F32)
         nc.gpsimd.memset(warm[:], 0.0)
         nc.scalar.activation(out=warm[:], in_=warm[:], func=ACT.Sigmoid)
@@ -88,22 +85,29 @@ def tile_grucell_e_kernel(
             nc.sync.dma_start(out=words_sb[:, v, :].bitcast(I32), in_=words[v].rearrange("p n t -> p (n t)").bitcast(I32))
 
         nc.sync.dma_start(out=hidden_sb[:], in_=hidden)
+        nc.sync.dma_start(out=x_pad[:, 0:N_VAR], in_=inputs)
         load_planes(gate_planes, gate_w_H2H_scales, 1)
-        for v in range(HALF, N_VAR):
+        for v in (4, 5):
+            load_words(gate_words, gate_w_H2H_words, v)
+        nc.sync.dma_start(out=r_small[0:32, :], in_=gate_w_I2H[HALF:N_VAR].rearrange("v o (m c) i -> (v o m) (c i)", c=P))
+        nc.sync.dma_start(out=r_small[32:64, :], in_=gate_bias[UNITS : 2 * UNITS].rearrange("(r c) -> r c", c=P))
+        for v in (6, 7):
+            load_words(gate_words, gate_w_H2H_words, v)
+        load_planes(gate_planes, gate_w_H2H_scales, 0)
+        for v in (0, 1):
             load_words(gate_words, gate_w_H2H_words, v)
         u_small = keep.tile([P, P], BF16)
         nc.vector.memset(u_small[:].bitcast(I32), 0)
-        nc.gpsimd.dma_start(out=z_rows[0:HALF, :], in_=gate_w_I2H[0:HALF].rearrange("v o c i -> v (o c i)"))
-        nc.gpsimd.dma_start(out=z_rows[ONES_ROW : ONES_ROW + HALF, :], in_=gate_bias[0:UNITS].rearrange("(r c) -> r c", r=HALF))
-        nc.gpsimd.dma_start(out=u_small[0:32, :], in_=update_w_I2H.rearrange("v o (m c) i -> (v o m) (c i)", c=P))
-        nc.gpsimd.dma_start(out=u_small[32:64, :], in_=update_bias.rearrange("(r c) -> r c", c=P))
-        load_planes(gate_planes, gate_w_H2H_scales, 0)
-        for v in range(HALF):
+        nc.sync.dma_start(out=z_rows[0:HALF, :], in_=gate_w_I2H[0:HALF].rearrange("v o c i -> v (o c i)"))
+        nc.sync.dma_start(out=z_rows[ONES_ROW : ONES_ROW + HALF, :], in_=gate_bias[0:UNITS].rearrange("(r c) -> r c", r=HALF))
+        nc.sync.dma_start(out=u_small[0:32, :], in_=update_w_I2H.rearrange("v o (m c) i -> (v o m) (c i)", c=P))
+        nc.sync.dma_start(out=u_small[32:64, :], in_=update_bias.rearrange("(r c) -> r c", c=P))
+        for v in (2, 3):
             load_words(gate_words, gate_w_H2H_words, v)
-        load_planes(update_planes, update_w_H2H_scales, 0)
-        load_planes(update_planes, update_w_H2H_scales, 1)
-        for v in range(N_VAR):
-            load_words(update_words, update_w_H2H_words, v)
+        for half in range(2):
+            load_planes(update_planes, update_w_H2H_scales, half)
+            for v in range(HALF * half, HALF * (half + 1)):
+                load_words(update_words, update_w_H2H_words, v)
 
         def by_variable(units):
             return units.rearrange("b (p t v) -> b v t p", t=PACK, v=N_VAR)
@@ -147,13 +151,24 @@ def tile_grucell_e_kernel(
             return back
 
         def columns_of(small, name):
-            turned = psum_k.tile([P, P], BF16, tag="k")
+            turned = psum.tile([P, P], BF16, tag="bank")
             nc.tensor.transpose(turned[:], small[:], ident_bf[:])
             columns = keep.tile([P, 64], F32, name=name)
             nc.vector.tensor_copy(out=columns[:], in_=turned[:, 0:64])
             return columns
 
-        x_all_t = psum_k.tile([P, N_VAR, P], BF16, tag="k")
+        h_grouped = keep.tile([P, N_VAR, P, PACK], BF16, align_bytes=64)
+        h_codes = keep.tile([P, N_VAR, P], U32, align_bytes=64)
+        h_planes = keep.tile([P, N_VAR, P], U8, align_bytes=64)
+        r_sorted = keep.tile([P, N_VAR, PACK, P], F32)
+
+        second = h_to_k(2)
+        third = h_to_k(3)
+        nc.vector.tensor_copy(out=h_grouped[:, 4:6], in_=second)
+        nc.scalar.copy(out=h_grouped[:, 6:8], in_=third)
+        quantise(h_grouped, 4, 2, h_codes, h_planes)
+
+        x_all_t = psum.tile([P, N_VAR, P], BF16, tag="bank")
         for v in range(N_VAR):
             nc.tensor.transpose(x_all_t[:, v, :], x_pad[:, v : v + 1].to_broadcast([P, P]), ident_bf[:])
         x_all = keep.tile([P, N_VAR, P], BF16)
@@ -166,11 +181,6 @@ def tile_grucell_e_kernel(
         for v in range(HALF):
             nc.vector.tensor_scalar(out=x_rows[:, v, :], in0=x_t[:], scalar1=mask[:, v : v + 1], scalar2=None, op0=ALU.mult)
         r_columns = columns_of(r_small, "r_columns")
-
-        h_grouped = keep.tile([P, N_VAR, P, PACK], BF16, align_bytes=64)
-        h_codes = keep.tile([P, N_VAR, P], U32, align_bytes=64)
-        h_planes = keep.tile([P, N_VAR, P], U8, align_bytes=64)
-        r_sorted = keep.tile([P, N_VAR, PACK, P], F32)
 
         def with_inputs(acc, v, wi, first_chunk):
             pre = work.tile([P, CHUNKS, P], F32)
@@ -193,11 +203,6 @@ def tile_grucell_e_kernel(
             these = slice(P_PER_BANK * k, P_PER_BANK * (k + 1))
             nc.scalar.activation(out=r_sorted[:, :, :, these], in_=by_variable(bank[:]), func=ACT.Sigmoid)
 
-        second = h_to_k(2)
-        third = h_to_k(3)
-        nc.vector.tensor_copy(out=h_grouped[:, 4:6], in_=second)
-        nc.scalar.copy(out=h_grouped[:, 6:8], in_=third)
-        quantise(h_grouped, 4, 2, h_codes, h_planes)
         r_started = {}
         for pair in range(5):
             if pair < 4:

@@ -21,6 +21,8 @@ BANK = 512
 N_BANKS = UNITS // BANK
 CHUNKS = BANK // P
 HALF = N_VAR // 2
+AFFINE_ON_VECTOR = (0, 1)
+AFFINE_ON_SCALAR = (2, 3)
 LAG = 3
 P_PER_BANK = BANK // (PACK * N_VAR)
 ONES_ROW = 16
@@ -86,11 +88,11 @@ def tile_grucell_e_kernel(
 
         nc.sync.dma_start(out=hidden_sb[:], in_=hidden)
         nc.sync.dma_start(out=x_pad[:, 0:N_VAR], in_=inputs)
-        load_planes(gate_planes, gate_w_H2H_scales, 1)
-        for v in (4, 5):
-            load_words(gate_words, gate_w_H2H_words, v)
         nc.sync.dma_start(out=r_small[0:32, :], in_=gate_w_I2H[HALF:N_VAR].rearrange("v o (m c) i -> (v o m) (c i)", c=P))
         nc.sync.dma_start(out=r_small[32:64, :], in_=gate_bias[UNITS : 2 * UNITS].rearrange("(r c) -> r c", c=P))
+        for v in (4, 5):
+            load_words(gate_words, gate_w_H2H_words, v)
+        load_planes(gate_planes, gate_w_H2H_scales, 1)
         for v in (6, 7):
             load_words(gate_words, gate_w_H2H_words, v)
         load_planes(gate_planes, gate_w_H2H_scales, 0)
@@ -162,25 +164,37 @@ def tile_grucell_e_kernel(
         h_planes = keep.tile([P, N_VAR, P], U8, align_bytes=64)
         r_sorted = keep.tile([P, N_VAR, PACK, P], F32)
 
-        second = h_to_k(2)
-        third = h_to_k(3)
-        nc.vector.tensor_copy(out=h_grouped[:, 4:6], in_=second)
-        nc.scalar.copy(out=h_grouped[:, 6:8], in_=third)
-        quantise(h_grouped, 4, 2, h_codes, h_planes)
 
         x_all_t = psum.tile([P, N_VAR, P], BF16, tag="bank")
         for v in range(N_VAR):
             nc.tensor.transpose(x_all_t[:, v, :], x_pad[:, v : v + 1].to_broadcast([P, P]), ident_bf[:])
         x_all = keep.tile([P, N_VAR, P], BF16)
         nc.scalar.copy(out=x_all[:], in_=x_all_t[:])
-        mask = keep.tile([P, HALF], F32)
-        nc.vector.tensor_tensor(out=mask[:], in0=ident_f32[:, 0:HALF], in1=ident_f32[:, ONES_ROW : ONES_ROW + HALF], op=ALU.add)
-        x_t = psum.tile([P, P], BF16, tag="bank")
-        nc.tensor.transpose(x_t[:], x_pad[:], ident_bf[:])
-        x_rows = keep.tile([P, HALF, P], BF16)
-        for v in range(HALF):
-            nc.vector.tensor_scalar(out=x_rows[:, v, :], in0=x_t[:], scalar1=mask[:, v : v + 1], scalar2=None, op0=ALU.mult)
         r_columns = columns_of(r_small, "r_columns")
+
+        r_affine = keep.tile([P, N_BANKS, CHUNKS, P], F32)
+
+        def affine_r(k):
+            for i in range(CHUNKS):
+                m = CHUNKS * k + i
+                wi = r_columns[:, m : m + 1]
+                bias = r_columns[:, 32 + m : 33 + m]
+                out_chunk = r_affine[:, k, i, :]
+                in_chunk = x_all[:, HALF + k // 2, :]
+                if k in AFFINE_ON_SCALAR:
+                    nc.scalar.activation(out=out_chunk, in_=in_chunk, func=ACT.Identity, scale=wi, bias=bias)
+                else:
+                    engine = nc.vector if k in AFFINE_ON_VECTOR else nc.gpsimd
+                    engine.tensor_scalar(out=out_chunk, in0=in_chunk, scalar1=wi, scalar2=bias, op0=ALU.mult, op1=ALU.add)
+
+        for k in (0, 2, 3, 4, 5, 6, 7):
+            affine_r(k)
+        second = h_to_k(2)
+        third = h_to_k(3)
+        nc.vector.tensor_copy(out=h_grouped[:, 4:6], in_=second)
+        nc.scalar.copy(out=h_grouped[:, 6:8], in_=third)
+        quantise(h_grouped, 4, 2, h_codes, h_planes)
+        affine_r(1)
 
         def with_inputs(acc, v, wi, first_chunk):
             pre = work.tile([P, CHUNKS, P], F32)
@@ -191,15 +205,12 @@ def tile_grucell_e_kernel(
 
         def start_r(k):
             acc = product_transposed(gate_words, gate_planes, HALF + k // 2, BANK * (k % 2), h_codes, h_planes)
-            return with_inputs(acc, HALF + k // 2, r_columns, CHUNKS * k)
+            r_t = work.tile([P, CHUNKS, P], F32)
+            nc.vector.tensor_tensor(out=r_t[:], in0=r_affine[:, k], in1=acc[:], op=ALU.add)
+            return r_t
 
-        def finish_r(k, pre):
-            bank = psum.tile([P, BANK], F32, tag="bank")
-            for i in range(CHUNKS):
-                chunk = bank[:, P * i : P * (i + 1)]
-                bias = r_columns[:, 32 + CHUNKS * k + i : 33 + CHUNKS * k + i]
-                nc.tensor.matmul(out=chunk, lhsT=bias.to_broadcast([P, P]), rhs=ident_f32[:], is_transpose=True, start=True, stop=False)
-                nc.tensor.matmul(out=chunk, lhsT=pre[:, i, :], rhs=ident_f32[:], is_transpose=True, start=False, stop=True)
+        def finish_r(k, r_t):
+            bank = transposed_back(r_t)
             these = slice(P_PER_BANK * k, P_PER_BANK * (k + 1))
             nc.scalar.activation(out=r_sorted[:, :, :, these], in_=by_variable(bank[:]), func=ACT.Sigmoid)
 
@@ -211,9 +222,15 @@ def tile_grucell_e_kernel(
             if pair == 0:
                 quantise(h_grouped, 6, 2, h_codes, h_planes)
             if pair == 3:
-                nc.vector.tensor_copy(out=h_grouped[:, 2:4], in_=first)
                 quantise(h_grouped, 0, 2, h_codes, h_planes)
-                u_columns = columns_of(u_small, "u_columns")
+                mask = keep.tile([P, HALF], F32)
+                nc.vector.tensor_tensor(out=mask[:], in0=ident_f32[:, 0:HALF], in1=ident_f32[:, ONES_ROW : ONES_ROW + HALF], op=ALU.add)
+                x_t = psum.tile([P, P], BF16, tag="bank")
+                nc.tensor.transpose(x_t[:], x_pad[:], ident_bf[:])
+                x_rows = keep.tile([P, HALF, P], BF16)
+                for v in range(HALF):
+                    nc.vector.tensor_scalar(out=x_rows[:, v, :], in0=x_t[:], scalar1=mask[:, v : v + 1], scalar2=None, op0=ALU.mult)
+                nc.vector.tensor_copy(out=h_grouped[:, 2:4], in_=first)
             if pair > 0:
                 finish_r(2 * pair - 2, r_started[2 * pair - 2])
                 finish_r(2 * pair - 1, r_started[2 * pair - 1])
@@ -222,6 +239,7 @@ def tile_grucell_e_kernel(
                 nc.scalar.copy(out=h_grouped[:, 0:2], in_=zeroth)
             if pair == 2:
                 first = h_to_k(1)
+                u_columns = columns_of(u_small, "u_columns")
         quantise(h_grouped, 2, 2, h_codes, h_planes)
 
         hr_grouped = keep.tile([P, N_VAR, P, PACK], BF16, align_bytes=64)
@@ -264,7 +282,7 @@ def tile_grucell_e_kernel(
             minus_new = work.tile([P, BANK], F32)
             nc.vector.scalar_tensor_tensor(out=minus_new[:], in0=zs[:, cols], scalar=1.0, in1=back[:], op0=ALU.subtract, op1=ALU.mult)
             result = work.tile([P, BANK], F32)
-            last_step = nc.vector if v in (3, 6, 7) else nc.gpsimd
+            last_step = nc.vector if v in (3, 5, 7) else nc.gpsimd
             last_step.tensor_tensor(out=result[:], in0=kept[:, cols], in1=minus_new[:], op=ALU.subtract)
             nc.sync.dma_start(out=out[:, cols], in_=result[:])
 

@@ -21,8 +21,7 @@ BANK = 512
 N_BANKS = UNITS // BANK
 CHUNKS = BANK // P
 HALF = N_VAR // 2
-AFFINE_ON_VECTOR = (0, 1)
-AFFINE_ON_SCALAR = (2, 3)
+AFFINE_ON_SCALAR = (0, 1, 4, 6)
 LAG = 3
 P_PER_BANK = BANK // (PACK * N_VAR)
 ONES_ROW = 16
@@ -152,11 +151,11 @@ def tile_grucell_e_kernel(
                 nc.tensor.transpose(back[:, P * i : P * (i + 1)], gate_t[:, i, :], ident_f32[:])
             return back
 
-        def columns_of(small, name):
+        def columns_of(small, name, copy):
             turned = psum.tile([P, P], BF16, tag="bank")
             nc.tensor.transpose(turned[:], small[:], ident_bf[:])
             columns = keep.tile([P, 64], F32, name=name)
-            nc.vector.tensor_copy(out=columns[:], in_=turned[:, 0:64])
+            copy(out=columns[:], in_=turned[:, 0:64])
             return columns
 
         h_grouped = keep.tile([P, N_VAR, P, PACK], BF16, align_bytes=64)
@@ -169,8 +168,8 @@ def tile_grucell_e_kernel(
         for v in range(N_VAR):
             nc.tensor.transpose(x_all_t[:, v, :], x_pad[:, v : v + 1].to_broadcast([P, P]), ident_bf[:])
         x_all = keep.tile([P, N_VAR, P], BF16)
-        nc.scalar.copy(out=x_all[:], in_=x_all_t[:])
-        r_columns = columns_of(r_small, "r_columns")
+        nc.vector.tensor_copy(out=x_all[:], in_=x_all_t[:])
+        r_columns = columns_of(r_small, "r_columns", nc.scalar.copy)
 
         r_affine = keep.tile([P, N_BANKS, CHUNKS, P], F32)
 
@@ -184,24 +183,7 @@ def tile_grucell_e_kernel(
                 if k in AFFINE_ON_SCALAR:
                     nc.scalar.activation(out=out_chunk, in_=in_chunk, func=ACT.Identity, scale=wi, bias=bias)
                 else:
-                    engine = nc.vector if k in AFFINE_ON_VECTOR else nc.gpsimd
-                    engine.tensor_scalar(out=out_chunk, in0=in_chunk, scalar1=wi, scalar2=bias, op0=ALU.mult, op1=ALU.add)
-
-        for k in (0, 2, 3, 4, 5, 6, 7):
-            affine_r(k)
-        second = h_to_k(2)
-        third = h_to_k(3)
-        nc.vector.tensor_copy(out=h_grouped[:, 4:6], in_=second)
-        nc.scalar.copy(out=h_grouped[:, 6:8], in_=third)
-        quantise(h_grouped, 4, 2, h_codes, h_planes)
-        affine_r(1)
-
-        def with_inputs(acc, v, wi, first_chunk):
-            pre = work.tile([P, CHUNKS, P], F32)
-            for i in range(CHUNKS):
-                scalar = wi[:, first_chunk + i : first_chunk + i + 1]
-                nc.vector.scalar_tensor_tensor(out=pre[:, i, :], in0=x_all[:, v, :], scalar=scalar, in1=acc[:, i, :], op0=ALU.mult, op1=ALU.add)
-            return pre
+                    nc.gpsimd.tensor_scalar(out=out_chunk, in0=in_chunk, scalar1=wi, scalar2=bias, op0=ALU.mult, op1=ALU.add)
 
         def start_r(k):
             acc = product_transposed(gate_words, gate_planes, HALF + k // 2, BANK * (k % 2), h_codes, h_planes)
@@ -214,33 +196,59 @@ def tile_grucell_e_kernel(
             these = slice(P_PER_BANK * k, P_PER_BANK * (k + 1))
             nc.scalar.activation(out=r_sorted[:, :, :, these], in_=by_variable(bank[:]), func=ACT.Sigmoid)
 
-        r_started = {}
-        for pair in range(5):
-            if pair < 4:
-                r_started[2 * pair] = start_r(2 * pair)
-                r_started[2 * pair + 1] = start_r(2 * pair + 1)
-            if pair == 0:
-                quantise(h_grouped, 6, 2, h_codes, h_planes)
-            if pair == 3:
-                quantise(h_grouped, 0, 2, h_codes, h_planes)
-                mask = keep.tile([P, HALF], F32)
-                nc.vector.tensor_tensor(out=mask[:], in0=ident_f32[:, 0:HALF], in1=ident_f32[:, ONES_ROW : ONES_ROW + HALF], op=ALU.add)
-                x_t = psum.tile([P, P], BF16, tag="bank")
-                nc.tensor.transpose(x_t[:], x_pad[:], ident_bf[:])
-                x_rows = keep.tile([P, HALF, P], BF16)
-                for v in range(HALF):
-                    nc.vector.tensor_scalar(out=x_rows[:, v, :], in0=x_t[:], scalar1=mask[:, v : v + 1], scalar2=None, op0=ALU.mult)
-                nc.vector.tensor_copy(out=h_grouped[:, 2:4], in_=first)
-            if pair > 0:
-                finish_r(2 * pair - 2, r_started[2 * pair - 2])
-                finish_r(2 * pair - 1, r_started[2 * pair - 1])
-            if pair == 1:
-                zeroth = h_to_k(0)
-                nc.scalar.copy(out=h_grouped[:, 0:2], in_=zeroth)
-            if pair == 2:
-                first = h_to_k(1)
-                u_columns = columns_of(u_small, "u_columns")
-        quantise(h_grouped, 2, 2, h_codes, h_planes)
+        def with_inputs(acc, v, wi, first_chunk):
+            pre = work.tile([P, CHUNKS, P], F32)
+            for i in range(CHUNKS):
+                scalar = wi[:, first_chunk + i : first_chunk + i + 1]
+                nc.vector.scalar_tensor_tensor(out=pre[:, i, :], in0=x_all[:, v, :], scalar=scalar, in1=acc[:, i, :], op0=ALU.mult, op1=ALU.add)
+            return pre
+
+        for k in range(N_BANKS):
+            if k not in AFFINE_ON_SCALAR:
+                affine_r(k)
+        affine_r(0)
+        second = h_to_k(2)
+        third = h_to_k(3)
+        nc.vector.tensor_copy(out=h_grouped[:, 4:5], in_=second[:, 0:1])
+        nc.scalar.copy(out=h_grouped[:, 5:6], in_=second[:, 1:2])
+        quantise(h_grouped, 4, 1, h_codes, h_planes)
+        nc.vector.tensor_copy(out=h_grouped[:, 6:7], in_=third[:, 0:1])
+        affine_r(1)
+        nc.scalar.copy(out=h_grouped[:, 7:8], in_=third[:, 1:2])
+        quantise(h_grouped, 5, 1, h_codes, h_planes)
+        r_t = {}
+        r_t[0] = start_r(0)
+        r_t[1] = start_r(1)
+        affine_r(4)
+        quantise(h_grouped, 6, 2, h_codes, h_planes)
+        r_t[2] = start_r(2)
+        r_t[3] = start_r(3)
+        finish_r(0, r_t[0])
+        finish_r(1, r_t[1])
+        affine_r(6)
+        r_t[4] = start_r(4)
+        r_t[5] = start_r(5)
+        finish_r(2, r_t[2])
+        finish_r(3, r_t[3])
+        r_t[6] = start_r(6)
+        r_t[7] = start_r(7)
+        zeroth = h_to_k(0)
+        nc.vector.tensor_copy(out=h_grouped[:, 0:2], in_=zeroth)
+        finish_r(4, r_t[4])
+        finish_r(5, r_t[5])
+        first = h_to_k(1)
+        finish_r(6, r_t[6])
+        finish_r(7, r_t[7])
+        nc.scalar.copy(out=h_grouped[:, 2:4], in_=first)
+        u_columns = columns_of(u_small, "u_columns", nc.vector.tensor_copy)
+        quantise(h_grouped, 0, 2, h_codes, h_planes)
+        mask = keep.tile([P, HALF], F32)
+        nc.vector.tensor_tensor(out=mask[:], in0=ident_f32[:, 0:HALF], in1=ident_f32[:, ONES_ROW : ONES_ROW + HALF], op=ALU.add)
+        x_t = psum.tile([P, P], BF16, tag="bank")
+        nc.tensor.transpose(x_t[:], x_pad[:], ident_bf[:])
+        x_rows = keep.tile([P, HALF, P], BF16)
+        for v in range(HALF):
+            nc.vector.tensor_scalar(out=x_rows[:, v, :], in0=x_t[:], scalar1=mask[:, v : v + 1], scalar2=None, op0=ALU.mult)
 
         hr_grouped = keep.tile([P, N_VAR, P, PACK], BF16, align_bytes=64)
         hr_codes = keep.tile([P, N_VAR, P], U32, align_bytes=64)
@@ -307,6 +315,8 @@ def tile_grucell_e_kernel(
             if step < N_VAR:
                 r_k = turn_r(step)
                 multiply_r(step, r_k)
+                if step == 0:
+                    quantise(h_grouped, 2, 2, h_codes, h_planes)
                 if step % 2 == 1:
                     quantise(hr_grouped, step - 1, 2, hr_codes, hr_planes)
             if 0 <= step - 1 < N_BANKS:

@@ -285,14 +285,24 @@ def tile_grucell_e_kernel(
             return g_t
 
         def finish_out(v, g_t):
-            cols = slice(BANK * v, BANK * (v + 1))
-            back = transposed_back(g_t)
-            minus_new = work.tile([P, BANK], F32)
-            nc.vector.scalar_tensor_tensor(out=minus_new[:], in0=zs[:, cols], scalar=1.0, in1=back[:], op0=ALU.subtract, op1=ALU.mult)
-            result = work.tile([P, BANK], F32)
-            last_step = nc.vector if v in (3, 5, 7) else nc.gpsimd
-            last_step.tensor_tensor(out=result[:], in0=kept[:, cols], in1=minus_new[:], op=ALU.subtract)
-            nc.sync.dma_start(out=out[:, cols], in_=result[:])
+            n_parts = 2 if v == N_VAR - 1 else 1
+            width = BANK // n_parts
+            halves = []
+            for part in range(n_parts):
+                cols = slice(BANK * v + width * part, BANK * v + width * (part + 1))
+                back = psum.tile([P, BANK], F32, tag="bank")
+                for i in range(width // P):
+                    nc.tensor.transpose(back[:, P * i : P * (i + 1)], g_t[:, width // P * part + i, :], ident_f32[:])
+                minus_new = work.tile([P, BANK], F32)
+                nc.vector.scalar_tensor_tensor(
+                    out=minus_new[:, 0:width], in0=zs[:, cols], scalar=1.0, in1=back[:, 0:width], op0=ALU.subtract, op1=ALU.mult
+                )
+                halves.append((cols, minus_new))
+            for cols, minus_new in halves:
+                result = work.tile([P, BANK], F32, bufs=6)
+                last_step = nc.vector if v >= HALF else nc.gpsimd
+                last_step.tensor_tensor(out=result[:, 0:width], in0=kept[:, cols], in1=minus_new[:, 0:width], op=ALU.subtract)
+                nc.sync.dma_start(out=out[:, cols], in_=result[:, 0:width])
 
         def turn_r(v):
             r_k = psum_k.tile([P, PACK, P], F32, tag="k")

@@ -20,8 +20,9 @@ UNITS = N_VAR * D
 BANK = 512
 N_BANKS = UNITS // BANK
 CHUNKS = BANK // P
+LAST = N_VAR - 1
 HALF = N_VAR // 2
-AFFINE_ON_SCALAR = (0, 1, 4, 6)
+AFFINE_ON_SCALAR = (0, 1, 2, 4, 6)
 LAG = 3
 P_PER_BANK = BANK // (PACK * N_VAR)
 ONES_ROW = 16
@@ -62,6 +63,8 @@ def tile_grucell_e_kernel(
         nc.vector.memset(gate_planes[:].rearrange("p g n -> p (g n)").bitcast(I32), 0)
         nc.vector.memset(update_planes[:].rearrange("p g n -> p (g n)").bitcast(I32), 0)
         nc.vector.memset(z_rows[:].bitcast(I32), 0)
+        last_rows = keep.tile([P, D], BF16)
+        nc.vector.memset(last_rows[:].bitcast(I32), 0)
         warm = keep.tile([P, 1], F32)
         nc.gpsimd.memset(warm[:], 0.0)
         nc.scalar.activation(out=warm[:], in_=warm[:], func=ACT.Sigmoid)
@@ -89,10 +92,9 @@ def tile_grucell_e_kernel(
         nc.sync.dma_start(out=x_pad[:, 0:N_VAR], in_=inputs)
         nc.sync.dma_start(out=r_small[0:32, :], in_=gate_w_I2H[HALF:N_VAR].rearrange("v o (m c) i -> (v o m) (c i)", c=P))
         nc.sync.dma_start(out=r_small[32:64, :], in_=gate_bias[UNITS : 2 * UNITS].rearrange("(r c) -> r c", c=P))
-        for v in (4, 5):
-            load_words(gate_words, gate_w_H2H_words, v)
+        load_words(gate_words, gate_w_H2H_words, HALF)
         load_planes(gate_planes, gate_w_H2H_scales, 1)
-        for v in (6, 7):
+        for v in range(HALF + 1, N_VAR):
             load_words(gate_words, gate_w_H2H_words, v)
         load_planes(gate_planes, gate_w_H2H_scales, 0)
         for v in (0, 1):
@@ -103,6 +105,8 @@ def tile_grucell_e_kernel(
         nc.sync.dma_start(out=z_rows[ONES_ROW : ONES_ROW + HALF, :], in_=gate_bias[0:UNITS].rearrange("(r c) -> r c", r=HALF))
         nc.sync.dma_start(out=u_small[0:32, :], in_=update_w_I2H.rearrange("v o (m c) i -> (v o m) (c i)", c=P))
         nc.sync.dma_start(out=u_small[32:64, :], in_=update_bias.rearrange("(r c) -> r c", c=P))
+        nc.sync.dma_start(out=last_rows[LAST:N_VAR, :], in_=update_w_I2H[LAST].rearrange("o c i -> o (c i)"))
+        nc.sync.dma_start(out=last_rows[ONES_ROW : ONES_ROW + 1, :], in_=update_bias[D * LAST : D * N_VAR].rearrange("(o c) -> o c", o=1))
         for v in (2, 3):
             load_words(gate_words, gate_w_H2H_words, v)
         for half in range(2):
@@ -219,12 +223,13 @@ def tile_grucell_e_kernel(
         r_t = {}
         r_t[0] = start_r(0)
         r_t[1] = start_r(1)
-        affine_r(4)
+        affine_r(2)
         quantise(h_grouped, 6, 2, h_codes, h_planes)
         r_t[2] = start_r(2)
         r_t[3] = start_r(3)
         finish_r(0, r_t[0])
         finish_r(1, r_t[1])
+        affine_r(4)
         affine_r(6)
         r_t[4] = start_r(4)
         r_t[5] = start_r(5)
@@ -242,12 +247,13 @@ def tile_grucell_e_kernel(
         nc.scalar.copy(out=h_grouped[:, 2:4], in_=first)
         u_columns = columns_of(u_small, "u_columns", nc.vector.tensor_copy)
         quantise(h_grouped, 0, 2, h_codes, h_planes)
-        mask = keep.tile([P, HALF], F32)
-        nc.vector.tensor_tensor(out=mask[:], in0=ident_f32[:, 0:HALF], in1=ident_f32[:, ONES_ROW : ONES_ROW + HALF], op=ALU.add)
+        mask = keep.tile([P, HALF + 1], F32)
+        nc.vector.tensor_tensor(out=mask[:, HALF:], in0=ident_f32[:, LAST:N_VAR], in1=ident_f32[:, ONES_ROW : ONES_ROW + 1], op=ALU.add)
+        nc.vector.tensor_tensor(out=mask[:, 0:HALF], in0=ident_f32[:, 0:HALF], in1=ident_f32[:, ONES_ROW : ONES_ROW + HALF], op=ALU.add)
         x_t = psum.tile([P, P], BF16, tag="bank")
         nc.tensor.transpose(x_t[:], x_pad[:], ident_bf[:])
-        x_rows = keep.tile([P, HALF, P], BF16)
-        for v in range(HALF):
+        x_rows = keep.tile([P, HALF + 1, P], BF16)
+        for v in range(HALF + 1):
             nc.vector.tensor_scalar(out=x_rows[:, v, :], in0=x_t[:], scalar1=mask[:, v : v + 1], scalar2=None, op0=ALU.mult)
 
         hr_grouped = keep.tile([P, N_VAR, P, PACK], BF16, align_bytes=64)
@@ -277,6 +283,10 @@ def tile_grucell_e_kernel(
 
         def start_out(v):
             acc = product_transposed(update_words, update_planes, v, 0, hr_codes, hr_planes)
+            if v == LAST:
+                raw = work.tile([P, CHUNKS, P], F32)
+                nc.scalar.copy(out=raw[:], in_=acc[:])
+                return raw
             pre = with_inputs(acc, v, u_columns, CHUNKS * v)
             g_t = work.tile([P, CHUNKS, P], F32)
             for i in range(CHUNKS):
@@ -284,25 +294,39 @@ def tile_grucell_e_kernel(
                 nc.scalar.activation(out=g_t[:, i, :], in_=pre[:, i, :], func=ACT.Tanh, bias=bias, scale=1.0)
             return g_t
 
+        def leave(cols, new, width):
+            minus_new = work.tile([P, BANK], F32)
+            nc.vector.scalar_tensor_tensor(
+                out=minus_new[:, 0:width], in0=zs[:, cols], scalar=1.0, in1=new, op0=ALU.subtract, op1=ALU.mult
+            )
+            return cols, minus_new, width
+
+        def store(cols, minus_new, width, engine):
+            result = work.tile([P, BANK], F32, bufs=6)
+            engine.tensor_tensor(out=result[:, 0:width], in0=kept[:, cols], in1=minus_new[:, 0:width], op=ALU.subtract)
+            nc.sync.dma_start(out=out[:, cols], in_=result[:, 0:width])
+
         def finish_out(v, g_t):
-            n_parts = 2 if v == N_VAR - 1 else 1
-            width = BANK // n_parts
+            cols = slice(BANK * v, BANK * (v + 1))
+            back = transposed_back(g_t)
+            store(*leave(cols, back[:], BANK), nc.vector if v >= HALF else nc.gpsimd)
+
+        def finish_last(raw):
+            width = BANK // 2
             halves = []
-            for part in range(n_parts):
-                cols = slice(BANK * v + width * part, BANK * v + width * (part + 1))
-                back = psum.tile([P, BANK], F32, tag="bank")
-                for i in range(width // P):
-                    nc.tensor.transpose(back[:, P * i : P * (i + 1)], g_t[:, width // P * part + i, :], ident_f32[:])
-                minus_new = work.tile([P, BANK], F32)
-                nc.vector.scalar_tensor_tensor(
-                    out=minus_new[:, 0:width], in0=zs[:, cols], scalar=1.0, in1=back[:, 0:width], op0=ALU.subtract, op1=ALU.mult
+            for part in range(2):
+                bank = psum.tile([P, BANK], F32, tag="bank")
+                nc.tensor.matmul(
+                    out=bank[:, 0:width], lhsT=x_rows[:, HALF, :], rhs=last_rows[:, width * part : width * (part + 1)], start=True, stop=False
                 )
-                halves.append((cols, minus_new))
-            for cols, minus_new in halves:
-                result = work.tile([P, BANK], F32, bufs=6)
-                last_step = nc.vector if v >= HALF else nc.gpsimd
-                last_step.tensor_tensor(out=result[:, 0:width], in0=kept[:, cols], in1=minus_new[:, 0:width], op=ALU.subtract)
-                nc.sync.dma_start(out=out[:, cols], in_=result[:, 0:width])
+                for i in range(2):
+                    chunk = bank[:, P * i : P * (i + 1)]
+                    nc.tensor.matmul(out=chunk, lhsT=raw[:, 2 * part + i, :], rhs=ident_f32[:], is_transpose=True, start=False, stop=i == 1)
+                new = work.tile([P, BANK], F32)
+                nc.scalar.activation(out=new[:, 0:width], in_=bank[:, 0:width], func=ACT.Tanh)
+                halves.append(leave(slice(BANK * LAST + width * part, BANK * LAST + width * (part + 1)), new[:, 0:width], width))
+            for half in halves:
+                store(*half, nc.vector)
 
         def turn_r(v):
             r_k = psum_k.tile([P, PACK, P], F32, tag="k")
@@ -316,20 +340,20 @@ def tile_grucell_e_kernel(
         z_started = {}
         out_started = {}
         for step in range(N_VAR + LAG + 1):
-            if 0 <= step < N_BANKS:
+            if step < N_BANKS:
                 z_started[step] = start_z(step)
             if 0 <= step - LAG < N_VAR:
                 out_started[step - LAG] = start_out(step - LAG)
             if 0 <= step - 1 < N_BANKS:
                 z_bank = open_z(step - 1)
             if step < N_VAR:
-                r_k = turn_r(step)
-                multiply_r(step, r_k)
+                multiply_r(step, turn_r(step))
                 if step == 0:
                     quantise(h_grouped, 2, 2, h_codes, h_planes)
                 if step % 2 == 1:
                     quantise(hr_grouped, step - 1, 2, hr_codes, hr_planes)
             if 0 <= step - 1 < N_BANKS:
                 finish_z(step - 1, z_started[step - 1], z_bank)
-            if 0 <= step - LAG - 1 < N_VAR:
+            if 0 <= step - LAG - 1 < LAST:
                 finish_out(step - LAG - 1, out_started[step - LAG - 1])
+        finish_last(out_started[LAST])

from contextlib import ExitStack

import concourse.mybir as mybir
from concourse.masks import make_identity

BF16 = mybir.dt.bfloat16
F32 = mybir.dt.float32
I32 = mybir.dt.int32
U32 = mybir.dt.uint32
U8 = mybir.dt.uint8
FP8X4 = mybir.dt.float8_e4m3fn_x4
ACT = mybir.ActivationFunctionType
ALU = mybir.AluOpType

P = 128
N_VAR = 8
D = 512
PACK = 4
UNITS = N_VAR * D
BANK = 512
N_BANKS = UNITS // BANK
CHUNKS = BANK // P
LAST = N_VAR - 1
HALF = N_VAR // 2
AFFINE_ON_SCALAR = (0, 1, 2, 4, 6)
LAG = 3
P_PER_BANK = BANK // (PACK * N_VAR)
ONES_ROW = 16

FLOPS = 2 * P * D * (3 * D) * N_VAR


def tile_grucell_e_kernel(
    tc,
    inputs,
    hidden,
    gate_w_I2H,
    gate_w_H2H_words,
    gate_w_H2H_scales,
    gate_bias,
    update_w_I2H,
    update_w_H2H_words,
    update_w_H2H_scales,
    update_bias,
    out,
):
    nc = tc.nc
    with ExitStack() as stack:
        stack.enter_context(tc.manual_schedule())
        keep = stack.enter_context(tc.tile_pool(name="keep", bufs=1))
        work = stack.enter_context(tc.tile_pool(name="work", bufs=4))
        psum_k = stack.enter_context(tc.psum_pool(name="psum_k", bufs=2))
        psum = stack.enter_context(tc.psum_pool(name="psum", bufs=6))

        gate_planes = keep.tile([P, 2, 2 * D], U8, align_bytes=64)
        update_planes = keep.tile([P, 2, D], U8, align_bytes=64)
        x_pad = keep.tile([P, P], BF16)
        z_rows = keep.tile([P, 2 * D], BF16)
        r_small = keep.tile([P, P], BF16)
        nc.vector.memset(x_pad[:], 0.0)
        nc.vector.memset(r_small[:].bitcast(I32), 0)
        nc.vector.memset(x_pad[:, ONES_ROW : ONES_ROW + HALF], 1.0)
        nc.vector.memset(gate_planes[:].rearrange("p g n -> p (g n)").bitcast(I32), 0)
        nc.vector.memset(update_planes[:].rearrange("p g n -> p (g n)").bitcast(I32), 0)
        nc.vector.memset(z_rows[:].bitcast(I32), 0)
        last_rows = keep.tile([P, D], BF16)
        nc.vector.memset(last_rows[:].bitcast(I32), 0)
        warm = keep.tile([P, 1], F32)
        nc.gpsimd.memset(warm[:], 0.0)
        nc.scalar.activation(out=warm[:], in_=warm[:], func=ACT.Sigmoid)

        ident_f32 = keep.tile([P, P], F32)
        make_identity(nc, ident_f32[:])
        ident_bf = keep.tile([P, P], BF16)
        nc.vector.tensor_copy(out=ident_bf[:], in_=ident_f32[:])

        hidden_sb = keep.tile([P, UNITS], BF16)
        gate_words = keep.tile([P, N_VAR, 2 * D], U32, align_bytes=64)
        update_words = keep.tile([P, N_VAR, D], U32, align_bytes=64)

        def load_planes(planes, scales, half):
            for quadrant in range(4):
                nc.sync.dma_start(
                    out=planes[32 * quadrant : 32 * quadrant + 16, half, :].bitcast(I32),
                    in_=scales[HALF * half : HALF * (half + 1), 4 * quadrant : 4 * quadrant + 4, :].bitcast(I32),
                )

        def load_words(words_sb, words, v):
            nc.sync.dma_start(out=words_sb[:, v, :].bitcast(I32), in_=words[v].rearrange("p n t -> p (n t)").bitcast(I32))

        nc.sync.dma_start(out=hidden_sb[:], in_=hidden)
        nc.sync.dma_start(out=x_pad[:, 0:N_VAR], in_=inputs)
        nc.sync.dma_start(out=r_small[0:32, :], in_=gate_w_I2H[HALF:N_VAR].rearrange("v o (m c) i -> (v o m) (c i)", c=P))
        nc.sync.dma_start(out=r_small[32:64, :], in_=gate_bias[UNITS : 2 * UNITS].rearrange("(r c) -> r c", c=P))
        load_words(gate_words, gate_w_H2H_words, HALF)
        load_planes(gate_planes, gate_w_H2H_scales, 1)
        for v in range(HALF + 1, N_VAR):
            load_words(gate_words, gate_w_H2H_words, v)
        load_planes(gate_planes, gate_w_H2H_scales, 0)
        for v in (0, 1):
            load_words(gate_words, gate_w_H2H_words, v)
        u_small = keep.tile([P, P], BF16)
        nc.vector.memset(u_small[:].bitcast(I32), 0)
        nc.sync.dma_start(out=z_rows[0:HALF, :], in_=gate_w_I2H[0:HALF].rearrange("v o c i -> v (o c i)"))
        nc.sync.dma_start(out=z_rows[ONES_ROW : ONES_ROW + HALF, :], in_=gate_bias[0:UNITS].rearrange("(r c) -> r c", r=HALF))
        nc.sync.dma_start(out=u_small[0:32, :], in_=update_w_I2H.rearrange("v o (m c) i -> (v o m) (c i)", c=P))
        nc.sync.dma_start(out=u_small[32:64, :], in_=update_bias.rearrange("(r c) -> r c", c=P))
        nc.sync.dma_start(out=last_rows[LAST:N_VAR, :], in_=update_w_I2H[LAST].rearrange("o c i -> o (c i)"))
        nc.sync.dma_start(out=last_rows[ONES_ROW : ONES_ROW + 1, :], in_=update_bias[D * LAST : D * N_VAR].rearrange("(o c) -> o c", o=1))
        for v in (2, 3):
            load_words(gate_words, gate_w_H2H_words, v)
        for half in range(2):
            load_planes(update_planes, update_w_H2H_scales, half)
            for v in range(HALF * half, HALF * (half + 1)):
                load_words(update_words, update_w_H2H_words, v)

        def by_variable(units):
            return units.rearrange("b (p t v) -> b v t p", t=PACK, v=N_VAR)

        h_words = hidden_sb[:].bitcast(F32).rearrange("b (p t w) -> b w t p", t=PACK, w=N_VAR // 2)

        def h_to_k(pair):
            k_first = psum_k.tile([P, PACK, P], F32, tag="k")
            for t in range(PACK):
                nc.tensor.transpose(k_first[:, t, :], h_words[:, pair, t, :], ident_f32[:])
            return k_first[:].bitcast(BF16).rearrange("p t (b i) -> p i b t", i=2)

        def quantise(grouped, first, count, codes, planes):
            these = slice(first, first + count)
            nc.vector.quantize_mx(
                out=codes[:, these, :].rearrange("p v b -> p (v b)").bitcast(FP8X4),
                scales=planes[:, these, :].rearrange("p v b -> p (v b)"),
                in_=grouped[:, these, :, :].rearrange("p v b t -> p (v b t)"),
            )

        def product_transposed(words, w_planes, v, first, codes, planes):
            acc = psum.tile([P, CHUNKS, P], F32, tag="bank")
            offset = 4 * (v % HALF)
            for i in range(CHUNKS):
                cols = slice(first + P * i, first + P * (i + 1))
                nc.tensor.matmul_mx(
                    out=acc[:, i, :],
                    lhsT=words[:, v, cols].bitcast(FP8X4),
                    lhsT_scale=w_planes[offset:P, v // HALF, cols],
                    rhs=codes[:, v, :].bitcast(FP8X4),
                    rhs_scale=planes[:, v, :],
                    start=True,
                    stop=True,
                )
            return acc

        def transposed_back(gate_t):
            back = psum.tile([P, BANK], F32, tag="bank")
            for i in range(CHUNKS):
                nc.tensor.transpose(back[:, P * i : P * (i + 1)], gate_t[:, i, :], ident_f32[:])
            return back

        def columns_of(small, name, copy):
            turned = psum.tile([P, P], BF16, tag="bank")
            nc.tensor.transpose(turned[:], small[:], ident_bf[:])
            columns = keep.tile([P, 64], F32, name=name)
            copy(out=columns[:], in_=turned[:, 0:64])
            return columns

        h_grouped = keep.tile([P, N_VAR, P, PACK], BF16, align_bytes=64)
        h_codes = keep.tile([P, N_VAR, P], U32, align_bytes=64)
        h_planes = keep.tile([P, N_VAR, P], U8, align_bytes=64)
        r_sorted = keep.tile([P, N_VAR, PACK, P], F32)


        x_all_t = psum.tile([P, N_VAR, P], BF16, tag="bank")
        for v in range(N_VAR):
            nc.tensor.transpose(x_all_t[:, v, :], x_pad[:, v : v + 1].to_broadcast([P, P]), ident_bf[:])
        x_all = keep.tile([P, N_VAR, P], BF16)
        nc.vector.tensor_copy(out=x_all[:], in_=x_all_t[:])
        r_columns = columns_of(r_small, "r_columns", nc.scalar.copy)

        r_affine = keep.tile([P, N_BANKS, CHUNKS, P], F32)

        def affine_r(k):
            for i in range(CHUNKS):
                m = CHUNKS * k + i
                wi = r_columns[:, m : m + 1]
                bias = r_columns[:, 32 + m : 33 + m]
                out_chunk = r_affine[:, k, i, :]
                in_chunk = x_all[:, HALF + k // 2, :]
                if k in AFFINE_ON_SCALAR:
                    nc.scalar.activation(out=out_chunk, in_=in_chunk, func=ACT.Identity, scale=wi, bias=bias)
                else:
                    nc.gpsimd.tensor_scalar(out=out_chunk, in0=in_chunk, scalar1=wi, scalar2=bias, op0=ALU.mult, op1=ALU.add)

        def start_r(k):
            acc = product_transposed(gate_words, gate_planes, HALF + k // 2, BANK * (k % 2), h_codes, h_planes)
            r_t = work.tile([P, CHUNKS, P], F32)
            nc.vector.tensor_tensor(out=r_t[:], in0=r_affine[:, k], in1=acc[:], op=ALU.add)
            return r_t

        def finish_r(k, r_t):
            bank = transposed_back(r_t)
            these = slice(P_PER_BANK * k, P_PER_BANK * (k + 1))
            nc.scalar.activation(out=r_sorted[:, :, :, these], in_=by_variable(bank[:]), func=ACT.Sigmoid)

        def with_inputs(acc, v, wi, first_chunk):
            pre = work.tile([P, CHUNKS, P], F32)
            for i in range(CHUNKS):
                scalar = wi[:, first_chunk + i : first_chunk + i + 1]
                nc.vector.scalar_tensor_tensor(out=pre[:, i, :], in0=x_all[:, v, :], scalar=scalar, in1=acc[:, i, :], op0=ALU.mult, op1=ALU.add)
            return pre

        for k in range(N_BANKS):
            if k not in AFFINE_ON_SCALAR:
                affine_r(k)
        affine_r(0)
        second = h_to_k(2)
        third = h_to_k(3)
        nc.vector.tensor_copy(out=h_grouped[:, 4:5], in_=second[:, 0:1])
        nc.scalar.copy(out=h_grouped[:, 5:6], in_=second[:, 1:2])
        quantise(h_grouped, 4, 1, h_codes, h_planes)
        nc.vector.tensor_copy(out=h_grouped[:, 6:7], in_=third[:, 0:1])
        affine_r(1)
        nc.scalar.copy(out=h_grouped[:, 7:8], in_=third[:, 1:2])
        quantise(h_grouped, 5, 1, h_codes, h_planes)
        r_t = {}
        r_t[0] = start_r(0)
        r_t[1] = start_r(1)
        affine_r(2)
        quantise(h_grouped, 6, 2, h_codes, h_planes)
        r_t[2] = start_r(2)
        r_t[3] = start_r(3)
        finish_r(0, r_t[0])
        finish_r(1, r_t[1])
        affine_r(4)
        affine_r(6)
        r_t[4] = start_r(4)
        r_t[5] = start_r(5)
        finish_r(2, r_t[2])
        finish_r(3, r_t[3])
        r_t[6] = start_r(6)
        r_t[7] = start_r(7)
        zeroth = h_to_k(0)
        nc.vector.tensor_copy(out=h_grouped[:, 0:2], in_=zeroth)
        finish_r(4, r_t[4])
        finish_r(5, r_t[5])
        first = h_to_k(1)
        finish_r(6, r_t[6])
        finish_r(7, r_t[7])
        nc.scalar.copy(out=h_grouped[:, 2:4], in_=first)
        u_columns = columns_of(u_small, "u_columns", nc.vector.tensor_copy)
        quantise(h_grouped, 0, 2, h_codes, h_planes)
        mask = keep.tile([P, HALF + 1], F32)
        nc.vector.tensor_tensor(out=mask[:, HALF:], in0=ident_f32[:, LAST:N_VAR], in1=ident_f32[:, ONES_ROW : ONES_ROW + 1], op=ALU.add)
        nc.vector.tensor_tensor(out=mask[:, 0:HALF], in0=ident_f32[:, 0:HALF], in1=ident_f32[:, ONES_ROW : ONES_ROW + HALF], op=ALU.add)
        x_t = psum.tile([P, P], BF16, tag="bank")
        nc.tensor.transpose(x_t[:], x_pad[:], ident_bf[:])
        x_rows = keep.tile([P, HALF + 1, P], BF16)
        for v in range(HALF + 1):
            nc.vector.tensor_scalar(out=x_rows[:, v, :], in0=x_t[:], scalar1=mask[:, v : v + 1], scalar2=None, op0=ALU.mult)

        hr_grouped = keep.tile([P, N_VAR, P, PACK], BF16, align_bytes=64)
        hr_codes = keep.tile([P, N_VAR, P], U32, align_bytes=64)
        hr_planes = keep.tile([P, N_VAR, P], U8, align_bytes=64)
        zs = keep.tile([P, UNITS], F32)
        kept = keep.tile([P, UNITS], F32)

        def start_z(k):
            acc = product_transposed(gate_words, gate_planes, k // 2, BANK * (k % 2), h_codes, h_planes)
            z_t = work.tile([P, CHUNKS, P], F32)
            nc.scalar.copy(out=z_t[:], in_=acc[:])
            return z_t

        def open_z(k):
            bank = psum.tile([P, BANK], F32, tag="bank")
            nc.tensor.matmul(out=bank[:], lhsT=x_rows[:, k // 2, :], rhs=z_rows[:, BANK * (k % 2) : BANK * (k % 2 + 1)], start=True, stop=False)
            return bank

        def finish_z(k, z_t, bank):
            cols = slice(BANK * k, BANK * (k + 1))
            for i in range(CHUNKS):
                chunk = bank[:, P * i : P * (i + 1)]
                nc.tensor.matmul(out=chunk, lhsT=z_t[:, i, :], rhs=ident_f32[:], is_transpose=True, start=False, stop=i == CHUNKS - 1)
            nc.scalar.activation(out=zs[:, cols], in_=bank[:], func=ACT.Sigmoid)
            nc.gpsimd.tensor_tensor(out=kept[:, cols], in0=zs[:, cols], in1=hidden_sb[:, cols], op=ALU.mult)

        def start_out(v):
            acc = product_transposed(update_words, update_planes, v, 0, hr_codes, hr_planes)
            if v == LAST:
                raw = work.tile([P, CHUNKS, P], F32)
                nc.scalar.copy(out=raw[:], in_=acc[:])
                return raw
            pre = with_inputs(acc, v, u_columns, CHUNKS * v)
            g_t = work.tile([P, CHUNKS, P], F32)
            for i in range(CHUNKS):
                bias = u_columns[:, 32 + CHUNKS * v + i : 33 + CHUNKS * v + i]
                nc.scalar.activation(out=g_t[:, i, :], in_=pre[:, i, :], func=ACT.Tanh, bias=bias, scale=1.0)
            return g_t

        def leave(cols, new, width):
            minus_new = work.tile([P, BANK], F32)
            nc.vector.scalar_tensor_tensor(
                out=minus_new[:, 0:width], in0=zs[:, cols], scalar=1.0, in1=new, op0=ALU.subtract, op1=ALU.mult
            )
            return cols, minus_new, width

        def store(cols, minus_new, width, engine):
            result = work.tile([P, BANK], F32, bufs=6)
            engine.tensor_tensor(out=result[:, 0:width], in0=kept[:, cols], in1=minus_new[:, 0:width], op=ALU.subtract)
            nc.sync.dma_start(out=out[:, cols], in_=result[:, 0:width])

        def finish_out(v, g_t):
            cols = slice(BANK * v, BANK * (v + 1))
            back = transposed_back(g_t)
            store(*leave(cols, back[:], BANK), nc.vector if v >= HALF else nc.gpsimd)

        def finish_last(raw):
            width = BANK // 2
            halves = []
            for part in range(2):
                bank = psum.tile([P, BANK], F32, tag="bank")
                nc.tensor.matmul(
                    out=bank[:, 0:width], lhsT=x_rows[:, HALF, :], rhs=last_rows[:, width * part : width * (part + 1)], start=True, stop=False
                )
                for i in range(2):
                    chunk = bank[:, P * i : P * (i + 1)]
                    nc.tensor.matmul(out=chunk, lhsT=raw[:, 2 * part + i, :], rhs=ident_f32[:], is_transpose=True, start=False, stop=i == 1)
                new = work.tile([P, BANK], F32)
                nc.scalar.activation(out=new[:, 0:width], in_=bank[:, 0:width], func=ACT.Tanh)
                halves.append(leave(slice(BANK * LAST + width * part, BANK * LAST + width * (part + 1)), new[:, 0:width], width))
            for half in halves:
                store(*half, nc.vector)

        def turn_r(v):
            r_k = psum_k.tile([P, PACK, P], F32, tag="k")
            for t in range(PACK):
                nc.tensor.transpose(r_k[:, t, :], r_sorted[:, v, t, :], ident_f32[:])
            return r_k

        def multiply_r(v, r_k):
            nc.vector.tensor_tensor(out=hr_grouped[:, v], in0=h_grouped[:, v], in1=r_k[:].rearrange("p t b -> p b t"), op=ALU.mult)

        z_started = {}
        out_started = {}
        for step in range(N_VAR + LAG + 1):
            if step < N_BANKS:
                z_started[step] = start_z(step)
            if 0 <= step - LAG < N_VAR:
                out_started[step - LAG] = start_out(step - LAG)
            if 0 <= step - 1 < N_BANKS:
                z_bank = open_z(step - 1)
            if step < N_VAR:
                multiply_r(step, turn_r(step))
                if step == 0:
                    quantise(h_grouped, 2, 2, h_codes, h_planes)
                if step % 2 == 1:
                    quantise(hr_grouped, step - 1, 2, hr_codes, hr_planes)
            if 0 <= step - 1 < N_BANKS:
                finish_z(step - 1, z_started[step - 1], z_bank)
            if 0 <= step - LAG - 1 < LAST:
                finish_out(step - LAG - 1, out_started[step - LAG - 1])
        finish_last(out_started[LAST])
